import numpy as np
import ml_dtypes


def mxq(x, axis, fmt="e4m3"):
    dtype, down = {"e4m3": (ml_dtypes.float8_e4m3fn, 7), "e5m2": (ml_dtypes.float8_e5m2, 14)}[fmt]
    v = np.moveaxis(np.asarray(x, np.float32).astype(ml_dtypes.bfloat16).astype(np.float64), axis, -1)
    blocks = v.reshape(v.shape[:-1] + (-1, 32))
    amax = np.abs(blocks).max(-1, keepdims=True)
    byte = np.maximum(np.where(amax > 0, np.frexp(amax)[1] - 1 + 127, 0) - down, 1)
    scale = np.exp2(byte - 127.0)
    codes = (blocks / scale).astype(np.float32).astype(dtype).astype(np.float64)
    return np.moveaxis((codes * scale).reshape(v.shape), -1, axis)


WIDE = False


def mx_kscale(k):
    if not WIDE:
        return np.ones(k)
    levels = np.array([10, -10, 5, -5, 0])
    a = np.random.permutation(np.resize(levels, k // 512 * 4)).reshape(k // 512, 4)
    idx = np.arange(k)
    return np.exp2(a[idx // 512, idx % 128 // 32])


BF16 = ml_dtypes.bfloat16


def bf(x):
    return np.asarray(x, np.float32).astype(BF16)


def f64(x):
    return np.asarray(x).astype(np.float64)


B, S, D, H, KA, LW = 2, 2048, 1024, 128, 3, 2
G = KA + 1
M = S // G
QS = np.sqrt(2.0 * np.sqrt(D / H))


def sparse_causal_mask(n, ka):
    i = np.arange(n)[:, None]
    j = np.arange(n)[None, :]
    local = np.abs(j - i) <= LW
    atrous = ((j - i) % (ka + 1) == 0) & ~((j == 0) & (i > 0))
    return (local | atrous) & (j <= i)


def classes(t):
    return t.reshape(B, M, G, H).transpose(0, 2, 1, 3)


def setup_inputs():
    s = mx_kscale(D)
    return {"q": bf(np.random.standard_normal((B, S, H)) * QS),
            "k_proj": bf(np.random.standard_normal((B, S, H)) * QS),
            "x": bf(np.random.standard_normal((B, S, D)) * s),
            "Wv": bf(np.random.standard_normal((H, D)) / np.sqrt(D) / s)}


def reference(q, k_proj, x, Wv):
    q, k_proj = f64(q), f64(k_proj)
    v = mxq(f64(x), 2, "e4m3") @ mxq(f64(Wv), 1, "e4m3").T
    mask = sparse_causal_mask(S, KA)
    keep = np.stack([mask[r::G, r::G] for r in range(G)])
    sa = classes(q) @ classes(k_proj).transpose(0, 1, 3, 2) / np.sqrt(D)
    sa = np.where(keep, sa, -np.inf)
    sl = np.full((LW, B, S), -np.inf)
    for d in range(1, LW + 1):
        sl[d - 1, :, d:] = (q[:, d:] * k_proj[:, :-d]).sum(-1) / np.sqrt(D)
    top = np.maximum(sa.max(-1).transpose(0, 2, 1).reshape(B, S), sl.max(0))
    ea = np.exp(sa - top.reshape(B, M, G).transpose(0, 2, 1)[..., None])
    el = np.exp(sl - top)
    num = mxq(ea, 3, "e4m3") @ mxq(classes(v), 2, "e4m3")
    num = num.transpose(0, 2, 1, 3).reshape(B, S, H)
    loc = np.zeros((B, S, H))
    for d in range(1, LW + 1):
        loc[:, d:] += el[d - 1, :, d:, None] * v[:, :-d]
    den = ea.sum(-1).transpose(0, 2, 1).reshape(B, S) + el.sum(0)
    return (num + loc) / den[..., None]

@@ -1,0 +1,472 @@
+from contextlib import ExitStack
+
+import concourse.mybir as mybir
+from concourse.masks import make_identity
+
+F32 = mybir.dt.float32
+BF16 = mybir.dt.bfloat16
+U32 = mybir.dt.uint32
+U8 = mybir.dt.uint8
+FP8X4 = mybir.dt.float8_e4m3fn_x4
+ALU = mybir.AluOpType
+ACT = mybir.ActivationFunctionType
+AX = mybir.AxisListType
+
+B, S, D, H = 2, 2048, 1024, 128
+G = 4
+LW = 2
+M = S // G
+P = 128
+MT = M // P
+NT = B * MT
+NC = B * G
+TILE_TOKENS = P * G
+PACK = 4
+K_PASS = P * PACK
+PASSES = D // K_PASS
+HALVES = 2
+WORDS = K_PASS // 2
+SCALE = 1.0 / 32.0
+MASKED = -1.0e30
+PAD = 8
+
+QUARTERS = NC * 4
+TILES = NC * MT
+BEHIND = G * MT
+
+FLOPS = 2 * B * S * D * H + 2 * (2 * B * G * M * M * H)
+
+
+def words_of(tile_2d):
+    return tile_2d.bitcast(F32)
+
+
+def tile_singlehead_pa_kernel(tc, q, k_proj, x, Wv, out):
+    nc = tc.nc
+    with ExitStack() as stack:
+        stack.enter_context(tc.manual_schedule())
+        const = stack.enter_context(tc.tile_pool(name="const", bufs=1))
+        x_pool = stack.enter_context(tc.tile_pool(name="x", bufs=NC))
+        pipe2 = stack.enter_context(tc.tile_pool(name="pipe2", bufs=2))
+        pipe3 = stack.enter_context(tc.tile_pool(name="pipe3", bufs=3))
+        small = stack.enter_context(tc.tile_pool(name="small", bufs=4))
+        psum_x = stack.enter_context(tc.psum_pool(name="psum_x", bufs=2))
+        psum_l = stack.enter_context(tc.psum_pool(name="psum_l", bufs=2))
+        psum_t = stack.enter_context(tc.psum_pool(name="psum_t", bufs=3))
+        psum_s = stack.enter_context(tc.psum_pool(name="psum_s", bufs=1))
+
+        q_tiles = q.flatten_outer_dims().rearrange("(T m r) h -> m T r h", T=NT, m=P, r=G)
+        k_rows = k_proj.flatten_outer_dims()
+        k_tiles = k_rows.rearrange("(T m r) h -> m T r h", T=NT, m=P, r=G)
+        x_tiles = x.flatten_outer_dims().rearrange("(T m r) k -> r m T k", T=NT, m=P, r=G)
+        out_tiles = out.flatten_outer_dims().rearrange("(T m r) h -> r m T h", T=NT, m=P, r=G)
+
+        ident_f = const.tile([P, P], F32)
+        make_identity(nc, ident_f[:])
+        ident_b = const.tile([P, P], BF16)
+        make_identity(nc, ident_b[:])
+        causal_f = const.tile([P, P], F32)
+        nc.gpsimd.memset(causal_f[:], 0.0)
+        nc.gpsimd.affine_select(
+            out=causal_f[:], in_=causal_f[:], pattern=[[-1, P]], compare_op=ALU.is_ge,
+            fill=MASKED, base=0, channel_multiplier=1,
+        )
+        causal_key0_f = const.tile([P, P], F32)
+        nc.gpsimd.affine_select(
+            out=causal_key0_f[:], in_=causal_f[:], pattern=[[P, P]], compare_op=ALU.is_ge,
+            fill=MASKED, base=0, channel_multiplier=-1,
+        )
+        causal = const.tile([P, P], BF16)
+        nc.vector.tensor_copy(out=causal[:], in_=causal_f[:])
+        causal_key0 = const.tile([P, P], BF16)
+        nc.vector.tensor_copy(out=causal_key0[:], in_=causal_key0_f[:])
+        key0 = const.tile([P, P], BF16)
+        nc.vector.memset(key0[:], 0.0)
+        nc.vector.memset(key0[:, 0:1], MASKED)
+
+        def mask_of(r, t, tk):
+            if r == 0 and tk == 0:
+                return causal_key0 if t == 0 else key0
+            return causal if tk == t else None
+
+        e_all = const.tile([P, 2, MT, M], BF16)
+        nc.vector.memset(e_all[:], 0.0)
+
+        wv_sb = const.tile([P, D], BF16)
+        nc.sync.dma_start(out=wv_sb[:], in_=Wv)
+        x_sb = []
+
+        def load_x(cls):
+            b, r = cls // G, cls % G
+            x_class = x_pool.tile([P, MT * D], BF16, tag="x")
+            nc.sync.dma_start(
+                out=x_class[:].rearrange("p (t k) -> p t k", t=MT), in_=x_tiles[r, :, b * MT : (b + 1) * MT, :]
+            )
+            x_sb.append(x_class)
+
+        load_x(0)
+        q_sb = const.tile([P, NT, G, H], BF16)
+        nc.sync.dma_start(out=q_sb[:], in_=q_tiles)
+        k_ext = const.tile([P, NT, LW + G, H], BF16)
+        nc.sync.dma_start(out=k_ext[:, :, LW:, :], in_=k_tiles)
+        early = k_rows[TILE_TOKENS - LW : TILE_TOKENS - LW + (NT - 1) * TILE_TOKENS, :].rearrange(
+            "(T m f) h -> m T f h", T=NT - 1, m=P, f=G
+        )
+        nc.sync.dma_start(out=k_ext[:, 1:, 0:LW, :], in_=early[:, :, 0:LW, :])
+        nc.vector.memset(k_ext[0:1, 0, 0:LW, :], 0.0)
+        first = k_rows[LW : LW + (P - 1) * G, :].rearrange("(m f) h -> m f h", f=G)
+        nc.sync.dma_start(out=k_ext[1:P, 0, 0:LW, :], in_=first[:, 0:LW, :])
+        for cls in range(1, NC):
+            load_x(cls)
+
+        def turn_words(bank, sources):
+            for i in range(2):
+                for u in range(HALVES):
+                    nc.tensor.transpose(bank[:, i, u, :], sources[i][:, u * P : (u + 1) * P], ident_f[:])
+
+        def copy_words(bank, grouped, pair):
+            grouped_words = words_of(grouped[:]).rearrange("p (c u) -> p c u", u=HALVES)
+            nc.scalar.copy(
+                out=grouped_words[:, 2 * P * pair : 2 * P * (pair + 1), :].rearrange("p (i m) u -> p i m u", i=2),
+                in_=bank[:].rearrange("p i u m -> p i m u"),
+            )
+
+        w_bank = psum_x.tile([P, PASSES, HALVES, H], F32, tag="xw")
+        wv_words = words_of(wv_sb[:])
+        turn_words(w_bank, [wv_words[:, g * WORDS : (g + 1) * WORDS] for g in range(PASSES)])
+        w_grouped = const.tile([P, PASSES * H * PACK], BF16, align_bytes=64)
+        copy_words(w_bank, w_grouped, 0)
+        w_codes = const.tile([P, PASSES, H], U32, align_bytes=64)
+        w_scales = const.tile([P, PASSES, H], U8, align_bytes=64)
+        nc.vector.quantize_mx(
+            out=w_codes[:].rearrange("p g h -> p (g h)").bitcast(FP8X4),
+            scales=w_scales[:].rearrange("p g h -> p (g h)"),
+            in_=w_grouped[:],
+        )
+
+        live = {}
+
+        def x_turn(k):
+            if not 0 <= k < QUARTERS:
+                return
+            cls, g, pair = k // 4, (k % 4) // 2, k % 2
+            x_words = words_of(x_sb[cls][:])
+            starts = [(2 * pair + i) * (D // 2) + g * WORDS for i in range(2)]
+            bank = psum_x.tile([P, 2, HALVES, P], F32, tag="xw")
+            turn_words(bank, [x_words[:, w0 : w0 + WORDS] for w0 in starts])
+            live["x_bank", k] = bank
+
+        def x_copy(k):
+            if not 0 <= k < QUARTERS:
+                return
+            if k % 2 == 0:
+                x_grouped = pipe3.tile([P, M * PACK], BF16, align_bytes=64)
+                live["x_grouped", k // 2] = x_grouped
+            copy_words(live["x_bank", k], live["x_grouped", k // 2], k % 2)
+
+        def x_quantise(k):
+            if not 0 <= k < QUARTERS or k % 2 != 1:
+                return
+            cls, g = k // 4, (k % 4) // 2
+            if g == 0:
+                x_codes = pipe2.tile([P, PASSES, M], U32, align_bytes=64)
+                x_scales = pipe2.tile([P, PASSES, M], U8, align_bytes=64)
+                live["x_codes", cls] = (x_codes, x_scales)
+            codes, scales = live["x_codes", cls]
+            nc.vector.quantize_mx(
+                out=codes[:, g, :].bitcast(FP8X4), scales=scales[:, g, :], in_=live["x_grouped", k // 2][:]
+            )
+
+        def v_project(k):
+            if not 0 <= k < QUARTERS or k % 4 != 3:
+                return
+            codes, scales = live["x_codes", k // 4]
+            vT_sum = psum_s.tile([P, M], F32, tag="sum")
+            for g in range(PASSES):
+                nc.tensor.matmul_mx(
+                    out=vT_sum[:],
+                    lhsT=w_codes[:, g, :].bitcast(FP8X4), lhsT_scale=w_scales[:, g, :],
+                    rhs=codes[:, g, :].bitcast(FP8X4), rhs_scale=scales[:, g, :],
+                    start=(g == 0), stop=(g == PASSES - 1),
+                )
+            live["vT_sum", k // 4] = vT_sum
+
+        def v_copy(k):
+            if not 0 <= k < QUARTERS or k % 4 != 3:
+                return
+            vT = pipe3.tile([P, PAD + M], F32)
+            nc.gpsimd.memset(vT[:, 0:PAD], 0.0)
+            nc.scalar.copy(out=vT[:, PAD:], in_=live["vT_sum", k // 4][:])
+            live["vT", k // 4] = vT
+
+        v_ext = const.tile([P, NT, LW + G, H], F32)
+        v_codes = const.tile([P, NC, H], U32, align_bytes=64)
+        v_scales = const.tile([P, NC, H], U8, align_bytes=64)
+
+        def v_turn_keys(k):
+            if not 0 <= k < QUARTERS or k % 4 != 3:
+                return
+            by_word = live["vT", k // 4][:, PAD:].rearrange("h (u p e) -> h u e p", u=HALVES, e=2)
+            v_bank = psum_t.tile([P, PACK, H], F32, tag="t")
+            for u in range(HALVES):
+                for e in range(2):
+                    nc.tensor.transpose(v_bank[:, 2 * u + e, :], by_word[:, u, e, :], ident_f[:])
+            live["v_bank", k // 4] = v_bank
+
+        def v_copy_keys(k):
+            if not 0 <= k < QUARTERS or k % 4 != 3:
+                return
+            v_grouped = pipe2.tile([P, H, PACK], BF16, align_bytes=64)
+            nc.scalar.copy(out=v_grouped[:], in_=live["v_bank", k // 4][:].rearrange("p j h -> p h j"))
+            live["v_grouped", k // 4] = v_grouped
+
+        def v_quantise(k):
+            if not 0 <= k < QUARTERS or k % 4 != 3:
+                return
+            nc.vector.quantize_mx(
+                out=v_codes[:, k // 4, :].bitcast(FP8X4), scales=v_scales[:, k // 4, :],
+                in_=live["v_grouped", k // 4][:].rearrange("p h j -> p (h j)"),
+            )
+
+        def has_rows(k, back):
+            return 0 <= k < QUARTERS and k % 4 == 3 and (back == 0 or (k // 4) % G >= G - LW)
+
+        def v_turn_rows(k, back):
+            if not has_rows(k, back):
+                return
+            rows = psum_t.tile([P, MT, H], F32, tag="t")
+            for t in range(MT):
+                n0 = PAD + t * P - back
+                nc.tensor.transpose(rows[:, t, :], live["vT", k // 4][:, n0 : n0 + P], ident_f[:])
+            live["v_rows", k // 4, back] = rows
+
+        def v_copy_rows(k, back):
+            if not has_rows(k, back):
+                return
+            b, r = (k // 4) // G, (k // 4) % G
+            nc.vector.tensor_copy(
+                out=v_ext[:, b * MT : (b + 1) * MT, LW + r - back * G, :], in_=live["v_rows", k // 4, back][:]
+            )
+
+        local_logit = const.tile([P, LW, NT, G], F32)
+        local_max = const.tile([P, NT, G], F32)
+
+        def local_logits(T):
+            products = []
+            for d in range(1, LW + 1):
+                product = pipe2.tile([P, G, H], F32, tag="product%d" % d)
+                nc.vector.tensor_tensor(
+                    out=product[:], in0=q_sb[:, T, :, :], in1=k_ext[:, T, LW - d : LW - d + G, :], op=ALU.mult
+                )
+                products.append(product)
+            for d in range(1, LW + 1):
+                nc.vector.reduce_sum(out=local_logit[:, d - 1, T, :], in_=products[d - 1][:], axis=AX.X)
+            if T % MT == 0:
+                nc.vector.memset(local_logit[0:1, 0, T, 0:1], MASKED)
+                nc.vector.memset(local_logit[0:1, 1, T, 0:2], MASKED)
+            nc.vector.tensor_max(out=local_max[:, T, :], in0=local_logit[:, 0, T, :], in1=local_logit[:, 1, T, :])
+
+        def qk_turn(i):
+            if not 0 <= i < TILES or i % MT != 0:
+                return
+            b, r = (i // MT) // G, (i // MT) % G
+            qk_bank = psum_t.tile([P, 2, MT, P], BF16, tag="t")
+            for t in range(MT):
+                nc.tensor.transpose(qk_bank[:, 0, t, :], q_sb[:, b * MT + t, r, :], ident_b[:])
+            for t in range(MT):
+                nc.tensor.transpose(qk_bank[:, 1, t, :], k_ext[:, b * MT + t, LW + r, :], ident_b[:])
+            live["qk_bank", i // MT] = qk_bank
+
+        def qk_copy(i):
+            if not 0 <= i < TILES or i % MT != 0:
+                return
+            qkT = pipe3.tile([P, 2, MT, P], BF16)
+            nc.scalar.copy(out=qkT[:], in_=live["qk_bank", i // MT][:])
+            live["qkT", i // MT] = qkT
+
+        def logits(i):
+            if not 0 <= i < TILES:
+                return
+            cls, t = i // MT, i % MT
+            qkT = live["qkT", cls]
+            bank = psum_l.tile([P, M], F32, tag="logits")
+            for tk in range(t + 1):
+                block = bank[:, tk * P : (tk + 1) * P]
+                mask = mask_of(cls % G, t, tk)
+                nc.tensor.matmul(out=block, lhsT=qkT[:, 0, t, :], rhs=qkT[:, 1, tk, :], start=True, stop=(mask is None))
+                if mask is not None:
+                    nc.tensor.matmul(out=block, lhsT=ident_b[:], rhs=mask[:], start=False, stop=True)
+            live["logits", i] = bank
+
+        def top(i):
+            if not 0 <= i < TILES:
+                return
+            cls, t = i // MT, i % MT
+            if t == 0:
+                row_max = small.tile([P, MT], F32)
+                neg_top = small.tile([P, MT], F32)
+                live["row_max", cls] = row_max
+                live["neg_top", cls] = neg_top
+            row_max, neg_top = live["row_max", cls], live["neg_top", cls]
+            nc.vector.reduce_max(out=row_max[:, t : t + 1], in_=live["logits", i][:, : (t + 1) * P], axis=AX.X)
+            nc.vector.tensor_scalar(
+                out=neg_top[:, t : t + 1], in0=row_max[:, t : t + 1],
+                scalar1=local_max[:, (cls // G) * MT + t, cls % G : cls % G + 1], scalar2=-SCALE,
+                op0=ALU.max, op1=ALU.mult,
+            )
+
+        def exponentials(i):
+            if not 0 <= i < TILES:
+                return
+            cls, t = i // MT, i % MT
+            if t == 0:
+                atrous_sum = small.tile([P, MT], F32)
+                live["atrous_sum", cls] = atrous_sum
+            keys = (t + 1) * P
+            nc.scalar.activation(
+                out=e_all[:, cls % 2, t, :keys], in_=live["logits", i][:, :keys], func=ACT.Exp,
+                bias=live["neg_top", cls][:, t : t + 1], scale=SCALE, accum_out=live["atrous_sum", cls][:, t : t + 1],
+            )
+
+        def e_turn(i):
+            if not 0 <= i < TILES or i % 2 != 1:
+                return
+            cls, t = i // MT, i % MT
+            bank = psum_t.tile([P, 2, HALVES, P], F32, tag="t")
+            turn_words(bank, [words_of(e_all[:, cls % 2, t - 1, :]), words_of(e_all[:, cls % 2, t, :])])
+            live["e_bank", i] = bank
+
+        def e_copy(i):
+            if not 0 <= i < TILES or i % 2 != 1:
+                return
+            cls, t = i // MT, i % MT
+            if t == 1:
+                e_grouped = pipe2.tile([P, M * PACK], BF16, align_bytes=64)
+                live["e_grouped", cls] = e_grouped
+            copy_words(live["e_bank", i], live["e_grouped", cls], t // 2)
+
+        def e_quantise(i):
+            if not 0 <= i < TILES or i % MT != MT - 1:
+                return
+            e_codes = pipe2.tile([P, M], U32, align_bytes=64)
+            e_scales = pipe2.tile([P, M], U8, align_bytes=64)
+            nc.vector.quantize_mx(out=e_codes[:].bitcast(FP8X4), scales=e_scales[:], in_=live["e_grouped", i // MT][:])
+            live["e_codes", i // MT] = (e_codes, e_scales)
+
+        def local_shift(i):
+            if not 0 <= i < TILES or i % MT != MT - 1:
+                return
+            cls = i // MT
+            b, r = cls // G, cls % G
+            shifted = small.tile([P, LW, MT], F32)
+            nc.vector.scalar_tensor_tensor(
+                out=shifted[:], in0=local_logit[:, :, b * MT : (b + 1) * MT, r], scalar=SCALE,
+                in1=live["neg_top", cls][:].unsqueeze(1).to_broadcast([P, LW, MT]), op0=ALU.mult, op1=ALU.add,
+            )
+            live["shifted", cls] = shifted
+
+        def local_exp(i):
+            if not 0 <= i < TILES or i % MT != MT - 1:
+                return
+            local_e = small.tile([P, LW, MT], F32)
+            nc.scalar.activation(out=local_e[:], in_=live["shifted", i // MT][:], func=ACT.Exp)
+            live["local_e", i // MT] = local_e
+
+        def denominators(i):
+            if not 0 <= i < TILES or i % MT != MT - 1:
+                return
+            cls = i // MT
+            local_e = live["local_e", cls]
+            den = small.tile([P, MT], F32)
+            nc.vector.tensor_add(out=den[:], in0=local_e[:, 0, :], in1=local_e[:, 1, :])
+            nc.vector.tensor_add(out=den[:], in0=den[:], in1=live["atrous_sum", cls][:])
+            inv_den = small.tile([P, MT], F32)
+            nc.vector.reciprocal(out=inv_den[:], in_=den[:])
+            local_w = small.tile([P, LW, MT], F32)
+            nc.vector.tensor_mul(
+                out=local_w[:], in0=local_e[:], in1=inv_den[:].unsqueeze(1).to_broadcast([P, LW, MT])
+            )
+            live["inv_den", cls] = inv_den
+            live["local_w", cls] = local_w
+
+        def atrous_product(i):
+            if not 0 <= i < TILES or i % MT != MT - 1:
+                return
+            cls = i // MT
+            e_codes, e_scales = live["e_codes", cls]
+            atrous = psum_s.tile([P, MT, H], F32, tag="sum")
+            for t in range(MT):
+                cols = slice(t * P, (t + 1) * P)
+                nc.tensor.matmul_mx(
+                    out=atrous[:, t, :],
+                    lhsT=e_codes[:, cols].bitcast(FP8X4), lhsT_scale=e_scales[:, cols],
+                    rhs=v_codes[:, cls, :].bitcast(FP8X4), rhs_scale=v_scales[:, cls, :],
+                    start=True, stop=True,
+                )
+            live["atrous", cls] = atrous
+
+        def atrous_scaled(i):
+            if not 0 <= i < TILES or i % MT != MT - 1:
+                return
+            cls = i // MT
+            part = pipe2.tile([P, MT, H], F32)
+            for t in range(MT):
+                nc.scalar.activation(
+                    out=part[:, t, :], in_=live["atrous", cls][:, t, :], func=ACT.Copy,
+                    scale=live["inv_den", cls][:, t : t + 1],
+                )
+            live["part", cls] = part
+
+        def add_local(i):
+            if not 0 <= i < TILES:
+                return
+            cls, t = i // MT, i % MT
+            b, r = cls // G, cls % G
+            if t == 0:
+                with_one = pipe2.tile([P, MT, H], F32)
+                result = pipe2.tile([P, MT, H], F32)
+                live["with_one", cls] = with_one
+                live["result", cls] = result
+            local_w = live["local_w", cls]
+            nc.vector.scalar_tensor_tensor(
+                out=live["with_one", cls][:, t, :], in0=v_ext[:, b * MT + t, LW + r - 1, :],
+                scalar=local_w[:, 0, t : t + 1], in1=live["part", cls][:, t, :], op0=ALU.mult, op1=ALU.add,
+            )
+            nc.vector.scalar_tensor_tensor(
+                out=live["result", cls][:, t, :], in0=v_ext[:, b * MT + t, LW + r - 2, :],
+                scalar=local_w[:, 1, t : t + 1], in1=live["with_one", cls][:, t, :], op0=ALU.mult, op1=ALU.add,
+            )
+            if t == MT - 1:
+                nc.sync.dma_start(out=out_tiles[r, :, b * MT : (b + 1) * MT, :], in_=live["result", cls][:])
+
+        LAST = BEHIND + TILES + 12
+        for step in range(LAST):
+            x_turn(step)
+            x_copy(step - 1)
+            x_quantise(step - 2)
+            v_project(step - 3)
+            v_copy(step - 4)
+            v_turn_keys(step - 5)
+            v_copy_keys(step - 6)
+            v_quantise(step - 7)
+            v_turn_rows(step - 6, 0)
+            v_copy_rows(step - 7, 0)
+            v_turn_rows(step - 7, 1)
+            v_copy_rows(step - 8, 1)
+            if step % MT == 0 and step // MT < NT:
+                local_logits(step // MT)
+            i = step - BEHIND
+            qk_turn(i + 5)
+            qk_copy(i + 4)
+            logits(i)
+            top(i - 1)
+            exponentials(i - 2)
+            e_turn(i - 3)
+            e_copy(i - 4)
+            e_quantise(i - 5)
+            atrous_product(i - 6)
+            atrous_scaled(i - 7)
+            local_shift(i - 2)
+            local_exp(i - 3)
+            denominators(i - 4)
+            add_local(i - 11)

@@ -261,6 +261,8 @@ def tile_singlehead_pa_kernel(tc, q, k_proj, x, Wv, out):
                 products.append(product)
             for d in range(1, LW + 1):
                 nc.vector.reduce_sum(out=local_logit[:, d - 1, T, :], in_=products[d - 1][:], axis=AX.X)
+
+        def local_maximum(T):
             if T % MT == 0:
                 nc.vector.memset(local_logit[0:1, 0, T, 0:1], MASKED)
                 nc.vector.memset(local_logit[0:1, 1, T, 0:2], MASKED)
@@ -298,19 +300,26 @@ def tile_singlehead_pa_kernel(tc, q, k_proj, x, Wv, out):
                     nc.tensor.matmul(out=block, lhsT=ident_b[:], rhs=mask[:], start=False, stop=True)
             live["logits", i] = bank
 
-        def top(i):
+        def row_maximum(i):
             if not 0 <= i < TILES:
                 return
             cls, t = i // MT, i % MT
             if t == 0:
                 row_max = small.tile([P, MT], F32)
-                neg_top = small.tile([P, MT], F32)
                 live["row_max", cls] = row_max
+            nc.vector.reduce_max(
+                out=live["row_max", cls][:, t : t + 1], in_=live["logits", i][:, : (t + 1) * P], axis=AX.X
+            )
+
+        def top(i):
+            if not 0 <= i < TILES:
+                return
+            cls, t = i // MT, i % MT
+            if t == 0:
+                neg_top = small.tile([P, MT], F32)
                 live["neg_top", cls] = neg_top
-            row_max, neg_top = live["row_max", cls], live["neg_top", cls]
-            nc.vector.reduce_max(out=row_max[:, t : t + 1], in_=live["logits", i][:, : (t + 1) * P], axis=AX.X)
             nc.vector.tensor_scalar(
-                out=neg_top[:, t : t + 1], in0=row_max[:, t : t + 1],
+                out=live["neg_top", cls][:, t : t + 1], in0=live["row_max", cls][:, t : t + 1],
                 scalar1=local_max[:, (cls // G) * MT + t, cls % G : cls % G + 1], scalar2=-SCALE,
                 op0=ALU.max, op1=ALU.mult,
             )
@@ -372,22 +381,37 @@ def tile_singlehead_pa_kernel(tc, q, k_proj, x, Wv, out):
             nc.scalar.activation(out=local_e[:], in_=live["shifted", i // MT][:], func=ACT.Exp)
             live["local_e", i // MT] = local_e
 
-        def denominators(i):
+        def local_sum(i):
             if not 0 <= i < TILES or i % MT != MT - 1:
                 return
-            cls = i // MT
-            local_e = live["local_e", cls]
+            local_e = live["local_e", i // MT]
+            local_den = small.tile([P, MT], F32)
+            nc.vector.tensor_add(out=local_den[:], in0=local_e[:, 0, :], in1=local_e[:, 1, :])
+            live["local_den", i // MT] = local_den
+
+        def denominator(i):
+            if not 0 <= i < TILES or i % MT != MT - 1:
+                return
             den = small.tile([P, MT], F32)
-            nc.vector.tensor_add(out=den[:], in0=local_e[:, 0, :], in1=local_e[:, 1, :])
-            nc.vector.tensor_add(out=den[:], in0=den[:], in1=live["atrous_sum", cls][:])
+            nc.vector.tensor_add(out=den[:], in0=live["local_den", i // MT][:], in1=live["atrous_sum", i // MT][:])
+            live["den", i // MT] = den
+
+        def inverse(i):
+            if not 0 <= i < TILES or i % MT != MT - 1:
+                return
             inv_den = small.tile([P, MT], F32)
-            nc.vector.reciprocal(out=inv_den[:], in_=den[:])
+            nc.vector.reciprocal(out=inv_den[:], in_=live["den", i // MT][:])
+            live["inv_den", i // MT] = inv_den
+
+        def local_weights(i):
+            if not 0 <= i < TILES or i % MT != MT - 1:
+                return
             local_w = small.tile([P, LW, MT], F32)
             nc.vector.tensor_mul(
-                out=local_w[:], in0=local_e[:], in1=inv_den[:].unsqueeze(1).to_broadcast([P, LW, MT])
+                out=local_w[:], in0=live["local_e", i // MT][:],
+                in1=live["inv_den", i // MT][:].unsqueeze(1).to_broadcast([P, LW, MT]),
             )
-            live["inv_den", cls] = inv_den
-            live["local_w", cls] = local_w
+            live["local_w", i // MT] = local_w
 
         def atrous_product(i):
             if not 0 <= i < TILES or i % MT != MT - 1:
@@ -417,30 +441,40 @@ def tile_singlehead_pa_kernel(tc, q, k_proj, x, Wv, out):
                 )
             live["part", cls] = part
 
-        def add_local(i):
+        def add_local_first(i):
             if not 0 <= i < TILES:
                 return
             cls, t = i // MT, i % MT
             b, r = cls // G, cls % G
             if t == 0:
                 with_one = pipe2.tile([P, MT, H], F32)
-                result = pipe2.tile([P, MT, H], F32)
                 live["with_one", cls] = with_one
-                live["result", cls] = result
-            local_w = live["local_w", cls]
             nc.vector.scalar_tensor_tensor(
                 out=live["with_one", cls][:, t, :], in0=v_ext[:, b * MT + t, LW + r - 1, :],
-                scalar=local_w[:, 0, t : t + 1], in1=live["part", cls][:, t, :], op0=ALU.mult, op1=ALU.add,
+                scalar=live["local_w", cls][:, 0, t : t + 1], in1=live["part", cls][:, t, :], op0=ALU.mult, op1=ALU.add,
             )
+
+        def add_local_second(i):
+            if not 0 <= i < TILES:
+                return
+            cls, t = i // MT, i % MT
+            b, r = cls // G, cls % G
+            if t == 0:
+                result = pipe2.tile([P, MT, H], F32)
+                live["result", cls] = result
             nc.vector.scalar_tensor_tensor(
                 out=live["result", cls][:, t, :], in0=v_ext[:, b * MT + t, LW + r - 2, :],
-                scalar=local_w[:, 1, t : t + 1], in1=live["with_one", cls][:, t, :], op0=ALU.mult, op1=ALU.add,
+                scalar=live["local_w", cls][:, 1, t : t + 1], in1=live["with_one", cls][:, t, :], op0=ALU.mult, op1=ALU.add,
             )
             if t == MT - 1:
                 nc.sync.dma_start(out=out_tiles[r, :, b * MT : (b + 1) * MT, :], in_=live["result", cls][:])
 
-        LAST = BEHIND + TILES + 12
+        LAST = BEHIND + TILES + 13
         for step in range(LAST):
+            i = step - BEHIND
+            row_maximum(i - 1)
+            add_local_first(i - 11)
+            add_local_second(i - 12)
             x_turn(step)
             x_copy(step - 1)
             x_quantise(step - 2)
@@ -455,11 +489,11 @@ def tile_singlehead_pa_kernel(tc, q, k_proj, x, Wv, out):
             v_copy_rows(step - 8, 1)
             if step % MT == 0 and step // MT < NT:
                 local_logits(step // MT)
-            i = step - BEHIND
+            if step % MT == 1 and step // MT < NT:
+                local_maximum(step // MT)
             qk_turn(i + 5)
             qk_copy(i + 4)
             logits(i)
-            top(i - 1)
             exponentials(i - 2)
             e_turn(i - 3)
             e_copy(i - 4)
@@ -468,5 +502,8 @@ def tile_singlehead_pa_kernel(tc, q, k_proj, x, Wv, out):
             atrous_scaled(i - 7)
             local_shift(i - 2)
             local_exp(i - 3)
-            denominators(i - 4)
-            add_local(i - 11)
+            local_sum(i - 4)
+            denominator(i - 5)
+            inverse(i - 6)
+            local_weights(i - 7)
+            top(i - 1)

@@ -94,30 +94,28 @@ def tile_singlehead_pa_kernel(tc, q, k_proj, x, Wv, out):
 
         wv_sb = const.tile([P, D], BF16)
         nc.sync.dma_start(out=wv_sb[:], in_=Wv)
-        x_sb = []
-
-        def load_x(cls):
-            b, r = cls // G, cls % G
-            x_class = x_pool.tile([P, MT * D], BF16, tag="x")
-            nc.sync.dma_start(
-                out=x_class[:].rearrange("p (t k) -> p t k", t=MT), in_=x_tiles[r, :, b * MT : (b + 1) * MT, :]
-            )
-            x_sb.append(x_class)
-
-        load_x(0)
         q_sb = const.tile([P, NT, G, H], BF16)
-        nc.sync.dma_start(out=q_sb[:], in_=q_tiles)
         k_ext = const.tile([P, NT, LW + G, H], BF16)
-        nc.sync.dma_start(out=k_ext[:, :, LW:, :], in_=k_tiles)
         early = k_rows[TILE_TOKENS - LW : TILE_TOKENS - LW + (NT - 1) * TILE_TOKENS, :].rearrange(
             "(T m f) h -> m T f h", T=NT - 1, m=P, f=G
         )
-        nc.sync.dma_start(out=k_ext[:, 1:, 0:LW, :], in_=early[:, :, 0:LW, :])
-        nc.vector.memset(k_ext[0:1, 0, 0:LW, :], 0.0)
         first = k_rows[LW : LW + (P - 1) * G, :].rearrange("(m f) h -> m f h", f=G)
-        nc.sync.dma_start(out=k_ext[1:P, 0, 0:LW, :], in_=first[:, 0:LW, :])
-        for cls in range(1, NC):
-            load_x(cls)
+        nc.vector.memset(k_ext[0:1, 0, 0:LW, :], 0.0)
+        x_sb = []
+        for b in range(B):
+            tiles_b = slice(b * MT, (b + 1) * MT)
+            nc.sync.dma_start(out=q_sb[:, tiles_b, :, :], in_=q_tiles[:, tiles_b, :, :])
+            nc.sync.dma_start(out=k_ext[:, tiles_b, LW:, :], in_=k_tiles[:, tiles_b, :, :])
+            if b == 0:
+                nc.sync.dma_start(out=k_ext[1:P, 0, 0:LW, :], in_=first[:, 0:LW, :])
+            after_first = slice(max(b * MT, 1), (b + 1) * MT)
+            nc.sync.dma_start(
+                out=k_ext[:, after_first, 0:LW, :], in_=early[:, max(b * MT, 1) - 1 : (b + 1) * MT - 1, 0:LW, :]
+            )
+            for r in range(G):
+                x_class = x_pool.tile([P, MT * D], BF16, tag="x")
+                nc.sync.dma_start(out=x_class[:].rearrange("p (t k) -> p t k", t=MT), in_=x_tiles[r, :, tiles_b, :])
+                x_sb.append(x_class)
 
         def turn_words(bank, sources):
             for i in range(2):
@@ -251,16 +249,17 @@ def tile_singlehead_pa_kernel(tc, q, k_proj, x, Wv, out):
         local_logit = const.tile([P, LW, NT, G], F32)
         local_max = const.tile([P, NT, G], F32)
 
-        def local_logits(T):
-            products = []
+        def local_products(T):
             for d in range(1, LW + 1):
                 product = pipe2.tile([P, G, H], F32, tag="product%d" % d)
-                nc.vector.tensor_tensor(
+                nc.gpsimd.tensor_tensor(
                     out=product[:], in0=q_sb[:, T, :, :], in1=k_ext[:, T, LW - d : LW - d + G, :], op=ALU.mult
                 )
-                products.append(product)
+                live["product", T, d] = product
+
+        def local_sums(T):
             for d in range(1, LW + 1):
-                nc.vector.reduce_sum(out=local_logit[:, d - 1, T, :], in_=products[d - 1][:], axis=AX.X)
+                nc.vector.reduce_sum(out=local_logit[:, d - 1, T, :], in_=live["product", T, d][:], axis=AX.X)
 
         def local_maximum(T):
             if T % MT == 0:
@@ -487,10 +486,13 @@ def tile_singlehead_pa_kernel(tc, q, k_proj, x, Wv, out):
             v_copy_rows(step - 7, 0)
             v_turn_rows(step - 7, 1)
             v_copy_rows(step - 8, 1)
-            if step % MT == 0 and step // MT < NT:
-                local_logits(step // MT)
-            if step % MT == 1 and step // MT < NT:
-                local_maximum(step // MT)
+            if step // MT < NT:
+                if step % MT == 0:
+                    local_products(step // MT)
+                if step % MT == 2:
+                    local_sums(step // MT)
+                if step % MT == 3:
+                    local_maximum(step // MT)
             qk_turn(i + 5)
             qk_copy(i + 4)
             logits(i)

@@ -50,10 +50,9 @@ def tile_singlehead_pa_kernel(tc, q, k_proj, x, Wv, out):
         pipe2 = stack.enter_context(tc.tile_pool(name="pipe2", bufs=2))
         pipe3 = stack.enter_context(tc.tile_pool(name="pipe3", bufs=3))
         small = stack.enter_context(tc.tile_pool(name="small", bufs=4))
-        psum_x = stack.enter_context(tc.psum_pool(name="psum_x", bufs=2))
-        psum_l = stack.enter_context(tc.psum_pool(name="psum_l", bufs=2))
+        psum_w = stack.enter_context(tc.psum_pool(name="psum_w", bufs=3))
         psum_t = stack.enter_context(tc.psum_pool(name="psum_t", bufs=3))
-        psum_s = stack.enter_context(tc.psum_pool(name="psum_s", bufs=1))
+        psum_s = stack.enter_context(tc.psum_pool(name="psum_s", bufs=2))
 
         q_tiles = q.flatten_outer_dims().rearrange("(T m r) h -> m T r h", T=NT, m=P, r=G)
         k_rows = k_proj.flatten_outer_dims()
@@ -129,7 +128,7 @@ def tile_singlehead_pa_kernel(tc, q, k_proj, x, Wv, out):
                 in_=bank[:].rearrange("p i u m -> p i m u"),
             )
 
-        w_bank = psum_x.tile([P, PASSES, HALVES, H], F32, tag="xw")
+        w_bank = psum_w.tile([P, PASSES, HALVES, H], F32, tag="w")
         wv_words = words_of(wv_sb[:])
         turn_words(w_bank, [wv_words[:, g * WORDS : (g + 1) * WORDS] for g in range(PASSES)])
         w_grouped = const.tile([P, PASSES * H * PACK], BF16, align_bytes=64)
@@ -150,7 +149,7 @@ def tile_singlehead_pa_kernel(tc, q, k_proj, x, Wv, out):
             cls, g, pair = k // 4, (k % 4) // 2, k % 2
             x_words = words_of(x_sb[cls][:])
             starts = [(2 * pair + i) * (D // 2) + g * WORDS for i in range(2)]
-            bank = psum_x.tile([P, 2, HALVES, P], F32, tag="xw")
+            bank = psum_w.tile([P, 2, HALVES, P], F32, tag="w")
             turn_words(bank, [x_words[:, w0 : w0 + WORDS] for w0 in starts])
             live["x_bank", k] = bank
 
@@ -248,6 +247,7 @@ def tile_singlehead_pa_kernel(tc, q, k_proj, x, Wv, out):
 
         local_logit = const.tile([P, LW, NT, G], F32)
         local_max = const.tile([P, NT, G], F32)
+        neg_local = const.tile([P, NT, G], F32)
 
         def local_products(T):
             for d in range(1, LW + 1):
@@ -266,6 +266,9 @@ def tile_singlehead_pa_kernel(tc, q, k_proj, x, Wv, out):
                 nc.vector.memset(local_logit[0:1, 0, T, 0:1], MASKED)
                 nc.vector.memset(local_logit[0:1, 1, T, 0:2], MASKED)
             nc.vector.tensor_max(out=local_max[:, T, :], in0=local_logit[:, 0, T, :], in1=local_logit[:, 1, T, :])
+
+        def local_negated(T):
+            nc.vector.tensor_scalar_mul(out=neg_local[:, T, :], in0=local_max[:, T, :], scalar1=-SCALE)
 
         def qk_turn(i):
             if not 0 <= i < TILES or i % MT != 0:
@@ -290,7 +293,7 @@ def tile_singlehead_pa_kernel(tc, q, k_proj, x, Wv, out):
                 return
             cls, t = i // MT, i % MT
             qkT = live["qkT", cls]
-            bank = psum_l.tile([P, M], F32, tag="logits")
+            bank = psum_w.tile([P, M], F32, tag="w")
             for tk in range(t + 1):
                 block = bank[:, tk * P : (tk + 1) * P]
                 mask = mask_of(cls % G, t, tk)
@@ -299,17 +302,6 @@ def tile_singlehead_pa_kernel(tc, q, k_proj, x, Wv, out):
                     nc.tensor.matmul(out=block, lhsT=ident_b[:], rhs=mask[:], start=False, stop=True)
             live["logits", i] = bank
 
-        def row_maximum(i):
-            if not 0 <= i < TILES:
-                return
-            cls, t = i // MT, i % MT
-            if t == 0:
-                row_max = small.tile([P, MT], F32)
-                live["row_max", cls] = row_max
-            nc.vector.reduce_max(
-                out=live["row_max", cls][:, t : t + 1], in_=live["logits", i][:, : (t + 1) * P], axis=AX.X
-            )
-
         def top(i):
             if not 0 <= i < TILES:
                 return
@@ -317,11 +309,14 @@ def tile_singlehead_pa_kernel(tc, q, k_proj, x, Wv, out):
             if t == 0:
                 neg_top = small.tile([P, MT], F32)
                 live["neg_top", cls] = neg_top
+            keys = (t + 1) * P
+            neg_scaled = pipe3.tile([P, M], F32)
             nc.vector.tensor_scalar(
-                out=live["neg_top", cls][:, t : t + 1], in0=live["row_max", cls][:, t : t + 1],
-                scalar1=local_max[:, (cls // G) * MT + t, cls % G : cls % G + 1], scalar2=-SCALE,
-                op0=ALU.max, op1=ALU.mult,
+                out=neg_scaled[:, :keys], in0=live["logits", i][:, :keys], scalar1=-SCALE,
+                scalar2=neg_local[:, (cls // G) * MT + t, cls % G : cls % G + 1], op0=ALU.mult, op1=ALU.min,
+                accum_out=live["neg_top", cls][:, t : t + 1],
             )
+            live["neg_scaled", i] = neg_scaled
 
         def exponentials(i):
             if not 0 <= i < TILES:
@@ -332,8 +327,8 @@ def tile_singlehead_pa_kernel(tc, q, k_proj, x, Wv, out):
                 live["atrous_sum", cls] = atrous_sum
             keys = (t + 1) * P
             nc.scalar.activation(
-                out=e_all[:, cls % 2, t, :keys], in_=live["logits", i][:, :keys], func=ACT.Exp,
-                bias=live["neg_top", cls][:, t : t + 1], scale=SCALE, accum_out=live["atrous_sum", cls][:, t : t + 1],
+                out=e_all[:, cls % 2, t, :keys], in_=live["neg_scaled", i][:, :keys], func=ACT.Exp,
+                bias=live["neg_top", cls][:, t : t + 1], scale=-1.0, accum_out=live["atrous_sum", cls][:, t : t + 1],
             )
 
         def e_turn(i):
@@ -471,7 +466,7 @@ def tile_singlehead_pa_kernel(tc, q, k_proj, x, Wv, out):
         LAST = BEHIND + TILES + 13
         for step in range(LAST):
             i = step - BEHIND
-            row_maximum(i - 1)
+            top(i - 1)
             add_local_first(i - 11)
             add_local_second(i - 12)
             x_turn(step)
@@ -493,6 +488,8 @@ def tile_singlehead_pa_kernel(tc, q, k_proj, x, Wv, out):
                     local_sums(step // MT)
                 if step % MT == 3:
                     local_maximum(step // MT)
+            if step % MT == 0 and 1 <= step // MT <= NT:
+                local_negated(step // MT - 1)
             qk_turn(i + 5)
             qk_copy(i + 4)
             logits(i)
@@ -508,4 +505,3 @@ def tile_singlehead_pa_kernel(tc, q, k_proj, x, Wv, out):
             denominator(i - 5)
             inverse(i - 6)
             local_weights(i - 7)
-            top(i - 1)

@@ -33,6 +33,8 @@ PAD = 8
 QUARTERS = NC * 4
 TILES = NC * MT
 BEHIND = G * MT
+FRONT_BEHIND = BEHIND - MT
+LOCAL_EVERY = FRONT_BEHIND // MT
 
 FLOPS = 2 * B * S * D * H + 2 * (2 * B * G * M * M * H)
 
@@ -100,8 +102,8 @@ def tile_singlehead_pa_kernel(tc, q, k_proj, x, Wv, out):
         )
         first = k_rows[LW : LW + (P - 1) * G, :].rearrange("(m f) h -> m f h", f=G)
         nc.vector.memset(k_ext[0:1, 0, 0:LW, :], 0.0)
-        x_sb = []
-        for b in range(B):
+
+        def load_q_k(b):
             tiles_b = slice(b * MT, (b + 1) * MT)
             nc.sync.dma_start(out=q_sb[:, tiles_b, :, :], in_=q_tiles[:, tiles_b, :, :])
             nc.sync.dma_start(out=k_ext[:, tiles_b, LW:, :], in_=k_tiles[:, tiles_b, :, :])
@@ -111,10 +113,18 @@ def tile_singlehead_pa_kernel(tc, q, k_proj, x, Wv, out):
             nc.sync.dma_start(
                 out=k_ext[:, after_first, 0:LW, :], in_=early[:, max(b * MT, 1) - 1 : (b + 1) * MT - 1, 0:LW, :]
             )
-            for r in range(G):
-                x_class = x_pool.tile([P, MT * D], BF16, tag="x")
-                nc.sync.dma_start(out=x_class[:].rearrange("p (t k) -> p t k", t=MT), in_=x_tiles[r, :, tiles_b, :])
-                x_sb.append(x_class)
+
+        x_sb = []
+        load_q_k(0)
+        for cls in range(NC):
+            x_class = x_pool.tile([P, MT * D], BF16, tag="x")
+            nc.sync.dma_start(
+                out=x_class[:].rearrange("p (t k) -> p t k", t=MT),
+                in_=x_tiles[cls % G, :, (cls // G) * MT : (cls // G + 1) * MT, :],
+            )
+            x_sb.append(x_class)
+            if cls == G:
+                load_q_k(1)
 
         def turn_words(bank, sources):
             for i in range(2):
@@ -249,7 +259,16 @@ def tile_singlehead_pa_kernel(tc, q, k_proj, x, Wv, out):
         local_max = const.tile([P, NT, G], F32)
         neg_local = const.tile([P, NT, G], F32)
 
-        def local_products(T):
+        def local_tile(s):
+            b, rest = s // BEHIND, s % BEHIND
+            if 0 <= b < B and rest % LOCAL_EVERY == 0 and rest // LOCAL_EVERY < MT:
+                return b * MT + rest // LOCAL_EVERY
+            return None
+
+        def local_products(s):
+            T = local_tile(s)
+            if T is None:
+                return
             for d in range(1, LW + 1):
                 product = pipe2.tile([P, G, H], F32, tag="product%d" % d)
                 nc.gpsimd.tensor_tensor(
@@ -257,17 +276,26 @@ def tile_singlehead_pa_kernel(tc, q, k_proj, x, Wv, out):
                 )
                 live["product", T, d] = product
 
-        def local_sums(T):
+        def local_sums(s):
+            T = local_tile(s)
+            if T is None:
+                return
             for d in range(1, LW + 1):
                 nc.vector.reduce_sum(out=local_logit[:, d - 1, T, :], in_=live["product", T, d][:], axis=AX.X)
 
-        def local_maximum(T):
+        def local_maximum(s):
+            T = local_tile(s)
+            if T is None:
+                return
             if T % MT == 0:
                 nc.vector.memset(local_logit[0:1, 0, T, 0:1], MASKED)
                 nc.vector.memset(local_logit[0:1, 1, T, 0:2], MASKED)
             nc.vector.tensor_max(out=local_max[:, T, :], in0=local_logit[:, 0, T, :], in1=local_logit[:, 1, T, :])
 
-        def local_negated(T):
+        def local_negated(s):
+            T = local_tile(s)
+            if T is None:
+                return
             nc.vector.tensor_scalar_mul(out=neg_local[:, T, :], in0=local_max[:, T, :], scalar1=-SCALE)
 
         def qk_turn(i):
@@ -465,10 +493,11 @@ def tile_singlehead_pa_kernel(tc, q, k_proj, x, Wv, out):
 
         LAST = BEHIND + TILES + 13
         for step in range(LAST):
-            i = step - BEHIND
+            i = step - FRONT_BEHIND
+            j = step - BEHIND
             top(i - 1)
-            add_local_first(i - 11)
-            add_local_second(i - 12)
+            add_local_first(j - 11)
+            add_local_second(j - 12)
             x_turn(step)
             x_copy(step - 1)
             x_quantise(step - 2)
@@ -481,15 +510,10 @@ def tile_singlehead_pa_kernel(tc, q, k_proj, x, Wv, out):
             v_copy_rows(step - 7, 0)
             v_turn_rows(step - 7, 1)
             v_copy_rows(step - 8, 1)
-            if step // MT < NT:
-                if step % MT == 0:
-                    local_products(step // MT)
-                if step % MT == 2:
-                    local_sums(step // MT)
-                if step % MT == 3:
-                    local_maximum(step // MT)
-            if step % MT == 0 and 1 <= step // MT <= NT:
-                local_negated(step // MT - 1)
+            local_products(step)
+            local_sums(step - 2)
+            local_maximum(step - 3)
+            local_negated(step - 4)
             qk_turn(i + 5)
             qk_copy(i + 4)
             logits(i)
@@ -497,8 +521,8 @@ def tile_singlehead_pa_kernel(tc, q, k_proj, x, Wv, out):
             e_turn(i - 3)
             e_copy(i - 4)
             e_quantise(i - 5)
-            atrous_product(i - 6)
-            atrous_scaled(i - 7)
+            atrous_product(j - 6)
+            atrous_scaled(j - 7)
             local_shift(i - 2)
             local_exp(i - 3)
             local_sum(i - 4)

@@ -25,16 +25,17 @@ PACK = 4
 K_PASS = P * PACK
 PASSES = D // K_PASS
 HALVES = 2
+PAIR = 2
 WORDS = K_PASS // 2
 SCALE = 1.0 / 32.0
 MASKED = -1.0e30
-PAD = 8
 
 QUARTERS = NC * 4
 TILES = NC * MT
 BEHIND = G * MT
 FRONT_BEHIND = BEHIND - MT
-LOCAL_EVERY = FRONT_BEHIND // MT
+LOCAL_BEHIND = 5
+LOCAL_EVERY = 2
 
 FLOPS = 2 * B * S * D * H + 2 * (2 * B * G * M * M * H)
 
@@ -52,8 +53,8 @@ def tile_singlehead_pa_kernel(tc, q, k_proj, x, Wv, out):
         pipe2 = stack.enter_context(tc.tile_pool(name="pipe2", bufs=2))
         pipe3 = stack.enter_context(tc.tile_pool(name="pipe3", bufs=3))
         small = stack.enter_context(tc.tile_pool(name="small", bufs=4))
-        psum_w = stack.enter_context(tc.psum_pool(name="psum_w", bufs=3))
-        psum_t = stack.enter_context(tc.psum_pool(name="psum_t", bufs=3))
+        psum_w = stack.enter_context(tc.psum_pool(name="psum_w", bufs=4))
+        psum_t = stack.enter_context(tc.psum_pool(name="psum_t", bufs=2))
         psum_s = stack.enter_context(tc.psum_pool(name="psum_s", bufs=2))
 
         q_tiles = q.flatten_outer_dims().rearrange("(T m r) h -> m T r h", T=NT, m=P, r=G)
@@ -91,10 +92,15 @@ def tile_singlehead_pa_kernel(tc, q, k_proj, x, Wv, out):
             return causal if tk == t else None
 
         e_all = const.tile([P, 2, MT, M], BF16)
-        nc.vector.memset(e_all[:], 0.0)
+        nc.vector.memset(e_all[:, :, 0:PAIR, M // 2 :], 0.0)
+        neg_even = {}
+        for t in range(0, MT, 2):
+            for i in range(2):
+                neg_tile = const.tile([P, (t + 2) * P], F32, name="neg_even_%d_%d" % (t, i))
+                nc.gpsimd.memset(neg_tile[:, (t + 1) * P :], -MASKED)
+                neg_even[t, i] = neg_tile
 
         wv_sb = const.tile([P, D], BF16)
-        nc.sync.dma_start(out=wv_sb[:], in_=Wv)
         q_sb = const.tile([P, NT, G, H], BF16)
         k_ext = const.tile([P, NT, LW + G, H], BF16)
         early = k_rows[TILE_TOKENS - LW : TILE_TOKENS - LW + (NT - 1) * TILE_TOKENS, :].rearrange(
@@ -115,14 +121,20 @@ def tile_singlehead_pa_kernel(tc, q, k_proj, x, Wv, out):
             )
 
         x_sb = []
-        load_q_k(0)
         for cls in range(NC):
             x_class = x_pool.tile([P, MT * D], BF16, tag="x")
-            nc.sync.dma_start(
-                out=x_class[:].rearrange("p (t k) -> p t k", t=MT),
-                in_=x_tiles[cls % G, :, (cls // G) * MT : (cls // G + 1) * MT, :],
-            )
+            pieces = 2 if cls == 0 else 1
+            for piece in range(pieces):
+                t0, t1 = piece * MT // pieces, (piece + 1) * MT // pieces
+                nc.sync.dma_start(
+                    out=x_class[:, t0 * D : t1 * D].rearrange("p (t k) -> p t k", t=t1 - t0),
+                    in_=x_tiles[cls % G, :, (cls // G) * MT + t0 : (cls // G) * MT + t1, :],
+                )
+                if cls == 0 and piece == 0:
+                    nc.sync.dma_start(out=wv_sb[:], in_=Wv)
             x_sb.append(x_class)
+            if cls == 1:
+                load_q_k(0)
             if cls == G:
                 load_q_k(1)
 
@@ -138,28 +150,39 @@ def tile_singlehead_pa_kernel(tc, q, k_proj, x, Wv, out):
                 in_=bank[:].rearrange("p i u m -> p i m u"),
             )
 
-        w_bank = psum_w.tile([P, PASSES, HALVES, H], F32, tag="w")
-        wv_words = words_of(wv_sb[:])
-        turn_words(w_bank, [wv_words[:, g * WORDS : (g + 1) * WORDS] for g in range(PASSES)])
         w_grouped = const.tile([P, PASSES * H * PACK], BF16, align_bytes=64)
-        copy_words(w_bank, w_grouped, 0)
         w_codes = const.tile([P, PASSES, H], U32, align_bytes=64)
         w_scales = const.tile([P, PASSES, H], U8, align_bytes=64)
-        nc.vector.quantize_mx(
-            out=w_codes[:].rearrange("p g h -> p (g h)").bitcast(FP8X4),
-            scales=w_scales[:].rearrange("p g h -> p (g h)"),
-            in_=w_grouped[:],
-        )
+
+        def w_turn(k):
+            if k != 1:
+                return
+            w_bank = psum_w.tile([P, PASSES, HALVES, H], F32, tag="w")
+            wv_words = words_of(wv_sb[:])
+            turn_words(w_bank, [wv_words[:, g * WORDS : (g + 1) * WORDS] for g in range(PASSES)])
+            live["w_bank"] = w_bank
+
+        def w_copy(k):
+            if k == 1:
+                copy_words(live["w_bank"], w_grouped, 0)
+
+        def w_quantise(k):
+            if k == 1:
+                nc.vector.quantize_mx(
+                    out=w_codes[:].rearrange("p g h -> p (g h)").bitcast(FP8X4),
+                    scales=w_scales[:].rearrange("p g h -> p (g h)"),
+                    in_=w_grouped[:],
+                )
 
         live = {}
 
         def x_turn(k):
             if not 0 <= k < QUARTERS:
                 return
-            cls, g, pair = k // 4, (k % 4) // 2, k % 2
+            cls, pair, g = k // 4, (k % 4) // 2, k % 2
             x_words = words_of(x_sb[cls][:])
             starts = [(2 * pair + i) * (D // 2) + g * WORDS for i in range(2)]
-            bank = psum_w.tile([P, 2, HALVES, P], F32, tag="w")
+            bank = psum_w.tile([P, PAIR, HALVES, P], F32, tag="w")
             turn_words(bank, [x_words[:, w0 : w0 + WORDS] for w0 in starts])
             live["x_bank", k] = bank
 
@@ -167,64 +190,56 @@ def tile_singlehead_pa_kernel(tc, q, k_proj, x, Wv, out):
             if not 0 <= k < QUARTERS:
                 return
             if k % 2 == 0:
-                x_grouped = pipe3.tile([P, M * PACK], BF16, align_bytes=64)
+                x_grouped = pipe3.tile([P, PASSES * PAIR * P * PACK], BF16, align_bytes=64)
                 live["x_grouped", k // 2] = x_grouped
             copy_words(live["x_bank", k], live["x_grouped", k // 2], k % 2)
 
         def x_quantise(k):
             if not 0 <= k < QUARTERS or k % 2 != 1:
                 return
-            cls, g = k // 4, (k % 4) // 2
-            if g == 0:
-                x_codes = pipe2.tile([P, PASSES, M], U32, align_bytes=64)
-                x_scales = pipe2.tile([P, PASSES, M], U8, align_bytes=64)
+            cls, pair = k // 4, (k % 4) // 2
+            if pair == 0:
+                x_codes = pipe2.tile([P, MT // PAIR, PASSES * PAIR * P], U32, align_bytes=64)
+                x_scales = pipe2.tile([P, MT // PAIR, PASSES * PAIR * P], U8, align_bytes=64)
                 live["x_codes", cls] = (x_codes, x_scales)
             codes, scales = live["x_codes", cls]
             nc.vector.quantize_mx(
-                out=codes[:, g, :].bitcast(FP8X4), scales=scales[:, g, :], in_=live["x_grouped", k // 2][:]
+                out=codes[:, pair, :].bitcast(FP8X4), scales=scales[:, pair, :], in_=live["x_grouped", k // 2][:]
             )
 
         def v_project(k):
             if not 0 <= k < QUARTERS or k % 4 != 3:
                 return
             codes, scales = live["x_codes", k // 4]
-            vT_sum = psum_s.tile([P, M], F32, tag="sum")
-            for g in range(PASSES):
-                nc.tensor.matmul_mx(
-                    out=vT_sum[:],
-                    lhsT=w_codes[:, g, :].bitcast(FP8X4), lhsT_scale=w_scales[:, g, :],
-                    rhs=codes[:, g, :].bitcast(FP8X4), rhs_scale=scales[:, g, :],
-                    start=(g == 0), stop=(g == PASSES - 1),
-                )
-            live["vT_sum", k // 4] = vT_sum
-
-        def v_copy(k):
-            if not 0 <= k < QUARTERS or k % 4 != 3:
-                return
-            vT = pipe3.tile([P, PAD + M], F32)
-            nc.gpsimd.memset(vT[:, 0:PAD], 0.0)
-            nc.scalar.copy(out=vT[:, PAD:], in_=live["vT_sum", k // 4][:])
-            live["vT", k // 4] = vT
+            v_sum = psum_s.tile([P, MT, H], F32, tag="sum")
+            for t in range(MT):
+                for g in range(PASSES):
+                    c0 = (g * PAIR + t % PAIR) * P
+                    nc.tensor.matmul_mx(
+                        out=v_sum[:, t, :],
+                        lhsT=codes[:, t // PAIR, c0 : c0 + P].bitcast(FP8X4), lhsT_scale=scales[:, t // PAIR, c0 : c0 + P],
+                        rhs=w_codes[:, g, :].bitcast(FP8X4), rhs_scale=w_scales[:, g, :],
+                        start=(g == 0), stop=(g == PASSES - 1),
+                    )
+            live["v_sum", k // 4] = v_sum
 
         v_ext = const.tile([P, NT, LW + G, H], F32)
+        for b in range(B):
+            nc.vector.memset(v_ext[0:1, b * MT, 0:LW, :], 0.0)
         v_codes = const.tile([P, NC, H], U32, align_bytes=64)
         v_scales = const.tile([P, NC, H], U8, align_bytes=64)
 
-        def v_turn_keys(k):
+        def v_copy_rows(k):
             if not 0 <= k < QUARTERS or k % 4 != 3:
                 return
-            by_word = live["vT", k // 4][:, PAD:].rearrange("h (u p e) -> h u e p", u=HALVES, e=2)
-            v_bank = psum_t.tile([P, PACK, H], F32, tag="t")
-            for u in range(HALVES):
-                for e in range(2):
-                    nc.tensor.transpose(v_bank[:, 2 * u + e, :], by_word[:, u, e, :], ident_f[:])
-            live["v_bank", k // 4] = v_bank
+            b, r = (k // 4) // G, (k // 4) % G
+            nc.scalar.copy(out=v_ext[:, b * MT : (b + 1) * MT, LW + r, :], in_=live["v_sum", k // 4][:])
 
         def v_copy_keys(k):
             if not 0 <= k < QUARTERS or k % 4 != 3:
                 return
             v_grouped = pipe2.tile([P, H, PACK], BF16, align_bytes=64)
-            nc.scalar.copy(out=v_grouped[:], in_=live["v_bank", k // 4][:].rearrange("p j h -> p h j"))
+            nc.scalar.copy(out=v_grouped[:], in_=live["v_sum", k // 4][:].rearrange("p j h -> p h j"))
             live["v_grouped", k // 4] = v_grouped
 
         def v_quantise(k):
@@ -235,24 +250,19 @@ def tile_singlehead_pa_kernel(tc, q, k_proj, x, Wv, out):
                 in_=live["v_grouped", k // 4][:].rearrange("p h j -> p (h j)"),
             )
 
-        def has_rows(k, back):
-            return 0 <= k < QUARTERS and k % 4 == 3 and (back == 0 or (k // 4) % G >= G - LW)
-
-        def v_turn_rows(k, back):
-            if not has_rows(k, back):
+        def v_shift(k):
+            if not 0 <= k < QUARTERS or k % BEHIND != BEHIND - 1:
                 return
-            rows = psum_t.tile([P, MT, H], F32, tag="t")
-            for t in range(MT):
-                n0 = PAD + t * P - back
-                nc.tensor.transpose(rows[:, t, :], live["vT", k // 4][:, n0 : n0 + P], ident_f[:])
-            live["v_rows", k // 4, back] = rows
-
-        def v_copy_rows(k, back):
-            if not has_rows(k, back):
-                return
-            b, r = (k // 4) // G, (k // 4) % G
-            nc.vector.tensor_copy(
-                out=v_ext[:, b * MT : (b + 1) * MT, LW + r - back * G, :], in_=live["v_rows", k // 4, back][:]
+            b = (k // 4) // G
+            tiles_b = slice(b * MT, (b + 1) * MT)
+            half = P // 2
+            for src, dst, n in ((0, 1, half), (half, half + 1, half - 1)):
+                nc.sync.dma_start(
+                    out=v_ext[dst : dst + n, tiles_b, 0:LW, :], in_=v_ext[src : src + n, tiles_b, G : G + LW, :]
+                )
+            nc.sync.dma_start(
+                out=v_ext[0:1, b * MT + 1 : (b + 1) * MT, 0:LW, :],
+                in_=v_ext[P - 1 : P, b * MT : (b + 1) * MT - 1, G : G + LW, :],
             )
 
         local_logit = const.tile([P, LW, NT, G], F32)
@@ -260,7 +270,7 @@ def tile_singlehead_pa_kernel(tc, q, k_proj, x, Wv, out):
         neg_local = const.tile([P, NT, G], F32)
 
         def local_tile(s):
-            b, rest = s // BEHIND, s % BEHIND
+            b, rest = (s - LOCAL_BEHIND) // BEHIND, (s - LOCAL_BEHIND) % BEHIND
             if 0 <= b < B and rest % LOCAL_EVERY == 0 and rest // LOCAL_EVERY < MT:
                 return b * MT + rest // LOCAL_EVERY
             return None
@@ -313,7 +323,7 @@ def tile_singlehead_pa_kernel(tc, q, k_proj, x, Wv, out):
             if not 0 <= i < TILES or i % MT != 0:
                 return
             qkT = pipe3.tile([P, 2, MT, P], BF16)
-            nc.scalar.copy(out=qkT[:], in_=live["qk_bank", i // MT][:])
+            nc.vector.tensor_copy(out=qkT[:], in_=live["qk_bank", i // MT][:])
             live["qkT", i // MT] = qkT
 
         def logits(i):
@@ -338,7 +348,10 @@ def tile_singlehead_pa_kernel(tc, q, k_proj, x, Wv, out):
                 neg_top = small.tile([P, MT], F32)
                 live["neg_top", cls] = neg_top
             keys = (t + 1) * P
-            neg_scaled = pipe3.tile([P, M], F32)
+            if t % 2 == 0:
+                neg_scaled = neg_even[t, cls % 2]
+            else:
+                neg_scaled = pipe3.tile([P, M], F32)
             nc.vector.tensor_scalar(
                 out=neg_scaled[:, :keys], in0=live["logits", i][:, :keys], scalar1=-SCALE,
                 scalar2=neg_local[:, (cls // G) * MT + t, cls % G : cls % G + 1], op0=ALU.mult, op1=ALU.min,
@@ -353,9 +366,10 @@ def tile_singlehead_pa_kernel(tc, q, k_proj, x, Wv, out):
             if t == 0:
                 atrous_sum = small.tile([P, MT], F32)
                 live["atrous_sum", cls] = atrous_sum
-            keys = (t + 1) * P
+            keys = (t // 2 + 1) * 2 * P
             nc.scalar.activation(
-                out=e_all[:, cls % 2, t, :keys], in_=live["neg_scaled", i][:, :keys], func=ACT.Exp,
+                out=e_all[:, cls % 2, t, :keys].rearrange("p (u m e) -> p u m e", e=2, m=P),
+                in_=live["neg_scaled", i][:, :keys].rearrange("p (u e m) -> p u m e", e=2, m=P), func=ACT.Exp,
                 bias=live["neg_top", cls][:, t : t + 1], scale=-1.0, accum_out=live["atrous_sum", cls][:, t : t + 1],
             )
 
@@ -491,25 +505,25 @@ def tile_singlehead_pa_kernel(tc, q, k_proj, x, Wv, out):
             if t == MT - 1:
                 nc.sync.dma_start(out=out_tiles[r, :, b * MT : (b + 1) * MT, :], in_=live["result", cls][:])
 
-        LAST = BEHIND + TILES + 13
+        LAST = BEHIND + TILES + 14
         for step in range(LAST):
             i = step - FRONT_BEHIND
             j = step - BEHIND
             top(i - 1)
-            add_local_first(j - 11)
-            add_local_second(j - 12)
+            add_local_first(j - 12)
+            add_local_second(j - 13)
+            w_turn(step)
             x_turn(step)
+            w_copy(step - 1)
             x_copy(step - 1)
+            w_quantise(step - 2)
             x_quantise(step - 2)
             v_project(step - 3)
-            v_copy(step - 4)
-            v_turn_keys(step - 5)
-            v_copy_keys(step - 6)
-            v_quantise(step - 7)
-            v_turn_rows(step - 6, 0)
-            v_copy_rows(step - 7, 0)
-            v_turn_rows(step - 7, 1)
-            v_copy_rows(step - 8, 1)
+            atrous_product(j - 7)
+            v_copy_rows(step - 4)
+            v_copy_keys(step - 4)
+            v_quantise(step - 5)
+            v_shift(step - 5)
             local_products(step)
             local_sums(step - 2)
             local_maximum(step - 3)
@@ -521,8 +535,7 @@ def tile_singlehead_pa_kernel(tc, q, k_proj, x, Wv, out):
             e_turn(i - 3)
             e_copy(i - 4)
             e_quantise(i - 5)
-            atrous_product(j - 6)
-            atrous_scaled(j - 7)
+            atrous_scaled(j - 8)
             local_shift(i - 2)
             local_exp(i - 3)
             local_sum(i - 4)

@@ -40,6 +40,10 @@ LOCAL_EVERY = 2
 FLOPS = 2 * B * S * D * H + 2 * (2 * B * G * M * M * H)
 
 
+def class_of(i):
+    return i // MT // G * G + (i // MT + LW) % G
+
+
 def words_of(tile_2d):
     return tile_2d.bitcast(F32)
 
@@ -311,25 +315,25 @@ def tile_singlehead_pa_kernel(tc, q, k_proj, x, Wv, out):
         def qk_turn(i):
             if not 0 <= i < TILES or i % MT != 0:
                 return
-            b, r = (i // MT) // G, (i // MT) % G
+            b, r = class_of(i) // G, class_of(i) % G
             qk_bank = psum_t.tile([P, 2, MT, P], BF16, tag="t")
             for t in range(MT):
                 nc.tensor.transpose(qk_bank[:, 0, t, :], q_sb[:, b * MT + t, r, :], ident_b[:])
             for t in range(MT):
                 nc.tensor.transpose(qk_bank[:, 1, t, :], k_ext[:, b * MT + t, LW + r, :], ident_b[:])
-            live["qk_bank", i // MT] = qk_bank
+            live["qk_bank", class_of(i)] = qk_bank
 
         def qk_copy(i):
             if not 0 <= i < TILES or i % MT != 0:
                 return
             qkT = pipe3.tile([P, 2, MT, P], BF16)
-            nc.vector.tensor_copy(out=qkT[:], in_=live["qk_bank", i // MT][:])
-            live["qkT", i // MT] = qkT
+            nc.vector.tensor_copy(out=qkT[:], in_=live["qk_bank", class_of(i)][:])
+            live["qkT", class_of(i)] = qkT
 
         def logits(i):
             if not 0 <= i < TILES:
                 return
-            cls, t = i // MT, i % MT
+            cls, t = class_of(i), i % MT
             qkT = live["qkT", cls]
             bank = psum_w.tile([P, M], F32, tag="w")
             for tk in range(t + 1):
@@ -343,7 +347,7 @@ def tile_singlehead_pa_kernel(tc, q, k_proj, x, Wv, out):
         def top(i):
             if not 0 <= i < TILES:
                 return
-            cls, t = i // MT, i % MT
+            cls, t = class_of(i), i % MT
             if t == 0:
                 neg_top = small.tile([P, MT], F32)
                 live["neg_top", cls] = neg_top
@@ -362,7 +366,7 @@ def tile_singlehead_pa_kernel(tc, q, k_proj, x, Wv, out):
         def exponentials(i):
             if not 0 <= i < TILES:
                 return
-            cls, t = i // MT, i % MT
+            cls, t = class_of(i), i % MT
             if t == 0:
                 atrous_sum = small.tile([P, MT], F32)
                 live["atrous_sum", cls] = atrous_sum
@@ -376,7 +380,7 @@ def tile_singlehead_pa_kernel(tc, q, k_proj, x, Wv, out):
         def e_turn(i):
             if not 0 <= i < TILES or i % 2 != 1:
                 return
-            cls, t = i // MT, i % MT
+            cls, t = class_of(i), i % MT
             bank = psum_t.tile([P, 2, HALVES, P], F32, tag="t")
             turn_words(bank, [words_of(e_all[:, cls % 2, t - 1, :]), words_of(e_all[:, cls % 2, t, :])])
             live["e_bank", i] = bank
@@ -384,7 +388,7 @@ def tile_singlehead_pa_kernel(tc, q, k_proj, x, Wv, out):
         def e_copy(i):
             if not 0 <= i < TILES or i % 2 != 1:
                 return
-            cls, t = i // MT, i % MT
+            cls, t = class_of(i), i % MT
             if t == 1:
                 e_grouped = pipe2.tile([P, M * PACK], BF16, align_bytes=64)
                 live["e_grouped", cls] = e_grouped
@@ -395,13 +399,13 @@ def tile_singlehead_pa_kernel(tc, q, k_proj, x, Wv, out):
                 return
             e_codes = pipe2.tile([P, M], U32, align_bytes=64)
             e_scales = pipe2.tile([P, M], U8, align_bytes=64)
-            nc.vector.quantize_mx(out=e_codes[:].bitcast(FP8X4), scales=e_scales[:], in_=live["e_grouped", i // MT][:])
-            live["e_codes", i // MT] = (e_codes, e_scales)
+            nc.vector.quantize_mx(out=e_codes[:].bitcast(FP8X4), scales=e_scales[:], in_=live["e_grouped", class_of(i)][:])
+            live["e_codes", class_of(i)] = (e_codes, e_scales)
 
         def local_shift(i):
             if not 0 <= i < TILES or i % MT != MT - 1:
                 return
-            cls = i // MT
+            cls = class_of(i)
             b, r = cls // G, cls % G
             shifted = small.tile([P, LW, MT], F32)
             nc.vector.scalar_tensor_tensor(
@@ -414,45 +418,45 @@ def tile_singlehead_pa_kernel(tc, q, k_proj, x, Wv, out):
             if not 0 <= i < TILES or i % MT != MT - 1:
                 return
             local_e = small.tile([P, LW, MT], F32)
-            nc.scalar.activation(out=local_e[:], in_=live["shifted", i // MT][:], func=ACT.Exp)
-            live["local_e", i // MT] = local_e
+            nc.scalar.activation(out=local_e[:], in_=live["shifted", class_of(i)][:], func=ACT.Exp)
+            live["local_e", class_of(i)] = local_e
 
         def local_sum(i):
             if not 0 <= i < TILES or i % MT != MT - 1:
                 return
-            local_e = live["local_e", i // MT]
+            local_e = live["local_e", class_of(i)]
             local_den = small.tile([P, MT], F32)
             nc.vector.tensor_add(out=local_den[:], in0=local_e[:, 0, :], in1=local_e[:, 1, :])
-            live["local_den", i // MT] = local_den
+            live["local_den", class_of(i)] = local_den
 
         def denominator(i):
             if not 0 <= i < TILES or i % MT != MT - 1:
                 return
             den = small.tile([P, MT], F32)
-            nc.vector.tensor_add(out=den[:], in0=live["local_den", i // MT][:], in1=live["atrous_sum", i // MT][:])
-            live["den", i // MT] = den
+            nc.vector.tensor_add(out=den[:], in0=live["local_den", class_of(i)][:], in1=live["atrous_sum", class_of(i)][:])
+            live["den", class_of(i)] = den
 
         def inverse(i):
             if not 0 <= i < TILES or i % MT != MT - 1:
                 return
             inv_den = small.tile([P, MT], F32)
-            nc.vector.reciprocal(out=inv_den[:], in_=live["den", i // MT][:])
-            live["inv_den", i // MT] = inv_den
+            nc.vector.reciprocal(out=inv_den[:], in_=live["den", class_of(i)][:])
+            live["inv_den", class_of(i)] = inv_den
 
         def local_weights(i):
             if not 0 <= i < TILES or i % MT != MT - 1:
                 return
             local_w = small.tile([P, LW, MT], F32)
             nc.vector.tensor_mul(
-                out=local_w[:], in0=live["local_e", i // MT][:],
-                in1=live["inv_den", i // MT][:].unsqueeze(1).to_broadcast([P, LW, MT]),
+                out=local_w[:], in0=live["local_e", class_of(i)][:],
+                in1=live["inv_den", class_of(i)][:].unsqueeze(1).to_broadcast([P, LW, MT]),
             )
-            live["local_w", i // MT] = local_w
+            live["local_w", class_of(i)] = local_w
 
         def atrous_product(i):
             if not 0 <= i < TILES or i % MT != MT - 1:
                 return
-            cls = i // MT
+            cls = class_of(i)
             e_codes, e_scales = live["e_codes", cls]
             atrous = psum_s.tile([P, MT, H], F32, tag="sum")
             for t in range(MT):
@@ -468,7 +472,7 @@ def tile_singlehead_pa_kernel(tc, q, k_proj, x, Wv, out):
         def atrous_scaled(i):
             if not 0 <= i < TILES or i % MT != MT - 1:
                 return
-            cls = i // MT
+            cls = class_of(i)
             part = pipe2.tile([P, MT, H], F32)
             for t in range(MT):
                 nc.scalar.activation(
@@ -480,7 +484,7 @@ def tile_singlehead_pa_kernel(tc, q, k_proj, x, Wv, out):
         def add_local_first(i):
             if not 0 <= i < TILES:
                 return
-            cls, t = i // MT, i % MT
+            cls, t = class_of(i), i % MT
             b, r = cls // G, cls % G
             if t == 0:
                 with_one = pipe2.tile([P, MT, H], F32)
@@ -493,7 +497,7 @@ def tile_singlehead_pa_kernel(tc, q, k_proj, x, Wv, out):
         def add_local_second(i):
             if not 0 <= i < TILES:
                 return
-            cls, t = i // MT, i % MT
+            cls, t = class_of(i), i % MT
             b, r = cls // G, cls % G
             if t == 0:
                 result = pipe2.tile([P, MT, H], F32)

@@ -118,7 +118,8 @@ def tile_singlehead_pa_kernel(tc, q, k_proj, x, Wv, out):
             nc.sync.dma_start(out=q_sb[:, tiles_b, :, :], in_=q_tiles[:, tiles_b, :, :])
             nc.sync.dma_start(out=k_ext[:, tiles_b, LW:, :], in_=k_tiles[:, tiles_b, :, :])
             if b == 0:
-                nc.sync.dma_start(out=k_ext[1:P, 0, 0:LW, :], in_=first[:, 0:LW, :])
+                nc.sync.dma_start(out=k_ext[1 : P - 1, 0, 0:LW, :], in_=first[: P - 2, 0:LW, :])
+                nc.sync.dma_start(out=k_ext[P - 1 : P, 0, 0:LW, :], in_=first[P - 2 :, 0:LW, :])
             after_first = slice(max(b * MT, 1), (b + 1) * MT)
             nc.sync.dma_start(
                 out=k_ext[:, after_first, 0:LW, :], in_=early[:, max(b * MT, 1) - 1 : (b + 1) * MT - 1, 0:LW, :]

@@ -34,8 +34,8 @@ QUARTERS = NC * 4
 TILES = NC * MT
 BEHIND = G * MT
 FRONT_BEHIND = BEHIND - MT
-LOCAL_BEHIND = 5
-LOCAL_EVERY = 2
+LOCAL_BEHIND = 4
+LOCAL_STEPS = 2 * MT
 
 FLOPS = 2 * B * S * D * H + 2 * (2 * B * G * M * M * H)
 
@@ -270,48 +270,32 @@ def tile_singlehead_pa_kernel(tc, q, k_proj, x, Wv, out):
                 in_=v_ext[P - 1 : P, b * MT : (b + 1) * MT - 1, G : G + LW, :],
             )
 
-        local_logit = const.tile([P, LW, NT, G], F32)
-        local_max = const.tile([P, NT, G], F32)
-        neg_local = const.tile([P, NT, G], F32)
+        neg_logit = const.tile([P, LW, B, G, MT], F32)
+        neg_local = const.tile([P, B, G, MT], F32)
 
-        def local_tile(s):
+        def local_logits(s):
             b, rest = (s - LOCAL_BEHIND) // BEHIND, (s - LOCAL_BEHIND) % BEHIND
-            if 0 <= b < B and rest % LOCAL_EVERY == 0 and rest // LOCAL_EVERY < MT:
-                return b * MT + rest // LOCAL_EVERY
-            return None
-
-        def local_products(s):
-            T = local_tile(s)
-            if T is None:
+            if not (0 <= b < B and rest < LOCAL_STEPS):
                 return
-            for d in range(1, LW + 1):
-                product = pipe2.tile([P, G, H], F32, tag="product%d" % d)
-                nc.gpsimd.tensor_tensor(
-                    out=product[:], in0=q_sb[:, T, :, :], in1=k_ext[:, T, LW - d : LW - d + G, :], op=ALU.mult
-                )
-                live["product", T, d] = product
+            t = rest // 2
+            T = b * MT + t
+            for r in (2 * (rest % 2), 2 * (rest % 2) + 1):
+                for d in range(1, LW + 1):
+                    product = pipe2.tile([P, H], F32)
+                    nc.vector.scalar_tensor_tensor(
+                        out=product[:], in0=q_sb[:, T, r, :], scalar=-SCALE, in1=k_ext[:, T, LW + r - d, :],
+                        op0=ALU.mult, op1=ALU.mult, accum_out=neg_logit[:, d - 1, b, r, t : t + 1],
+                    )
 
-        def local_sums(s):
-            T = local_tile(s)
-            if T is None:
+        def local_minimum(s):
+            b, rest = (s - LOCAL_BEHIND) // BEHIND, (s - LOCAL_BEHIND) % BEHIND
+            if not (0 <= b < B and rest == LOCAL_STEPS):
                 return
-            for d in range(1, LW + 1):
-                nc.vector.reduce_sum(out=local_logit[:, d - 1, T, :], in_=live["product", T, d][:], axis=AX.X)
-
-        def local_maximum(s):
-            T = local_tile(s)
-            if T is None:
-                return
-            if T % MT == 0:
-                nc.vector.memset(local_logit[0:1, 0, T, 0:1], MASKED)
-                nc.vector.memset(local_logit[0:1, 1, T, 0:2], MASKED)
-            nc.vector.tensor_max(out=local_max[:, T, :], in0=local_logit[:, 0, T, :], in1=local_logit[:, 1, T, :])
-
-        def local_negated(s):
-            T = local_tile(s)
-            if T is None:
-                return
-            nc.vector.tensor_scalar_mul(out=neg_local[:, T, :], in0=local_max[:, T, :], scalar1=-SCALE)
+            nc.vector.memset(neg_logit[0:1, :, b, 0, 0:1], -MASKED)
+            nc.vector.memset(neg_logit[0:1, 1, b, 1, 0:1], -MASKED)
+            nc.vector.tensor_tensor(
+                out=neg_local[:, b, :, :], in0=neg_logit[:, 0, b, :, :], in1=neg_logit[:, 1, b, :, :], op=ALU.min
+            )
 
         def qk_turn(i):
             if not 0 <= i < TILES or i % MT != 0:
@@ -359,7 +343,7 @@ def tile_singlehead_pa_kernel(tc, q, k_proj, x, Wv, out):
                 neg_scaled = pipe3.tile([P, M], F32)
             nc.vector.tensor_scalar(
                 out=neg_scaled[:, :keys], in0=live["logits", i][:, :keys], scalar1=-SCALE,
-                scalar2=neg_local[:, (cls // G) * MT + t, cls % G : cls % G + 1], op0=ALU.mult, op1=ALU.min,
+                scalar2=neg_local[:, cls // G, cls % G, t : t + 1], op0=ALU.mult, op1=ALU.min,
                 accum_out=live["neg_top", cls][:, t : t + 1],
             )
             live["neg_scaled", i] = neg_scaled
@@ -369,13 +353,13 @@ def tile_singlehead_pa_kernel(tc, q, k_proj, x, Wv, out):
                 return
             cls, t = class_of(i), i % MT
             if t == 0:
-                atrous_sum = small.tile([P, MT], F32)
-                live["atrous_sum", cls] = atrous_sum
+                e_sums = small.tile([P, 1 + LW, MT], F32)
+                live["e_sums", cls] = e_sums
             keys = (t // 2 + 1) * 2 * P
             nc.scalar.activation(
                 out=e_all[:, cls % 2, t, :keys].rearrange("p (u m e) -> p u m e", e=2, m=P),
                 in_=live["neg_scaled", i][:, :keys].rearrange("p (u e m) -> p u m e", e=2, m=P), func=ACT.Exp,
-                bias=live["neg_top", cls][:, t : t + 1], scale=-1.0, accum_out=live["atrous_sum", cls][:, t : t + 1],
+                bias=live["neg_top", cls][:, t : t + 1], scale=-1.0, accum_out=live["e_sums", cls][:, 0, t : t + 1],
             )
 
         def e_turn(i):
@@ -407,34 +391,25 @@ def tile_singlehead_pa_kernel(tc, q, k_proj, x, Wv, out):
             if not 0 <= i < TILES or i % MT != MT - 1:
                 return
             cls = class_of(i)
-            b, r = cls // G, cls % G
             shifted = small.tile([P, LW, MT], F32)
-            nc.vector.scalar_tensor_tensor(
-                out=shifted[:], in0=local_logit[:, :, b * MT : (b + 1) * MT, r], scalar=SCALE,
-                in1=live["neg_top", cls][:].unsqueeze(1).to_broadcast([P, LW, MT]), op0=ALU.mult, op1=ALU.add,
+            nc.vector.tensor_sub(
+                out=shifted[:], in0=live["neg_top", cls][:].unsqueeze(1).to_broadcast([P, LW, MT]),
+                in1=neg_logit[:, :, cls // G, cls % G, :],
             )
             live["shifted", cls] = shifted
 
         def local_exp(i):
             if not 0 <= i < TILES or i % MT != MT - 1:
                 return
-            local_e = small.tile([P, LW, MT], F32)
-            nc.scalar.activation(out=local_e[:], in_=live["shifted", class_of(i)][:], func=ACT.Exp)
-            live["local_e", class_of(i)] = local_e
-
-        def local_sum(i):
-            if not 0 <= i < TILES or i % MT != MT - 1:
-                return
-            local_e = live["local_e", class_of(i)]
-            local_den = small.tile([P, MT], F32)
-            nc.vector.tensor_add(out=local_den[:], in0=local_e[:, 0, :], in1=local_e[:, 1, :])
-            live["local_den", class_of(i)] = local_den
+            nc.scalar.activation(
+                out=live["e_sums", class_of(i)][:, 1:, :], in_=live["shifted", class_of(i)][:], func=ACT.Exp
+            )
 
         def denominator(i):
             if not 0 <= i < TILES or i % MT != MT - 1:
                 return
             den = small.tile([P, MT], F32)
-            nc.vector.tensor_add(out=den[:], in0=live["local_den", class_of(i)][:], in1=live["atrous_sum", class_of(i)][:])
+            nc.vector.reduce_sum(out=den[:], in_=live["e_sums", class_of(i)][:].rearrange("p s t -> p t s"), axis=AX.X)
             live["den", class_of(i)] = den
 
         def inverse(i):
@@ -449,7 +424,7 @@ def tile_singlehead_pa_kernel(tc, q, k_proj, x, Wv, out):
                 return
             local_w = small.tile([P, LW, MT], F32)
             nc.vector.tensor_mul(
-                out=local_w[:], in0=live["local_e", class_of(i)][:],
+                out=local_w[:], in0=live["e_sums", class_of(i)][:, 1:, :],
                 in1=live["inv_den", class_of(i)][:].unsqueeze(1).to_broadcast([P, LW, MT]),
             )
             live["local_w", class_of(i)] = local_w
@@ -529,10 +504,8 @@ def tile_singlehead_pa_kernel(tc, q, k_proj, x, Wv, out):
             v_copy_keys(step - 4)
             v_quantise(step - 5)
             v_shift(step - 5)
-            local_products(step)
-            local_sums(step - 2)
-            local_maximum(step - 3)
-            local_negated(step - 4)
+            local_logits(step)
+            local_minimum(step)
             qk_turn(i + 5)
             qk_copy(i + 4)
             logits(i)
@@ -543,7 +516,6 @@ def tile_singlehead_pa_kernel(tc, q, k_proj, x, Wv, out):
             atrous_scaled(j - 8)
             local_shift(i - 2)
             local_exp(i - 3)
-            local_sum(i - 4)
-            denominator(i - 5)
-            inverse(i - 6)
-            local_weights(i - 7)
+            denominator(i - 4)
+            inverse(i - 5)
+            local_weights(i - 6)

@@ -32,9 +32,9 @@ MASKED = -1.0e30
 
 QUARTERS = NC * 4
 TILES = NC * MT
-BEHIND = G * MT
-FRONT_BEHIND = BEHIND - MT
-LOCAL_BEHIND = 4
+SEQUENCE = G * MT
+BEHIND = SEQUENCE - MT
+LOCAL_BEHIND = 5
 LOCAL_STEPS = 2 * MT
 
 FLOPS = 2 * B * S * D * H + 2 * (2 * B * G * M * M * H)
@@ -42,6 +42,23 @@ FLOPS = 2 * B * S * D * H + 2 * (2 * B * G * M * M * H)
 
 def class_of(i):
     return i // MT // G * G + (i // MT + LW) % G
+
+
+def tile_of(i):
+    return i % MT
+
+
+def pair_of(i):
+    t = tile_of(i) // PAIR * PAIR
+    return [t, t + 1]
+
+
+def piece_of(i):
+    if not 0 <= i < TILES:
+        return []
+    if i >= TILES - MT:
+        return pair_of(i) if i % PAIR == PAIR - 1 else []
+    return list(range(MT)) if i % MT == MT - 1 else []
 
 
 def words_of(tile_2d):
@@ -56,9 +73,11 @@ def tile_singlehead_pa_kernel(tc, q, k_proj, x, Wv, out):
         x_pool = stack.enter_context(tc.tile_pool(name="x", bufs=NC))
         pipe2 = stack.enter_context(tc.tile_pool(name="pipe2", bufs=2))
         pipe3 = stack.enter_context(tc.tile_pool(name="pipe3", bufs=3))
-        small = stack.enter_context(tc.tile_pool(name="small", bufs=4))
+        results = stack.enter_context(tc.tile_pool(name="results", bufs=NC))
+        small = stack.enter_context(tc.tile_pool(name="small", bufs=6))
         psum_w = stack.enter_context(tc.psum_pool(name="psum_w", bufs=4))
-        psum_t = stack.enter_context(tc.psum_pool(name="psum_t", bufs=2))
+        psum_e = stack.enter_context(tc.psum_pool(name="psum_e", bufs=1))
+        psum_t = stack.enter_context(tc.psum_pool(name="psum_t", bufs=1))
         psum_s = stack.enter_context(tc.psum_pool(name="psum_s", bufs=2))
 
         q_tiles = q.flatten_outer_dims().rearrange("(T m r) h -> m T r h", T=NT, m=P, r=G)
@@ -143,9 +162,9 @@ def tile_singlehead_pa_kernel(tc, q, k_proj, x, Wv, out):
             if cls == G:
                 load_q_k(1)
 
-        def turn_words(bank, sources):
+        def turn_words(bank, sources, halves=range(HALVES)):
             for i in range(2):
-                for u in range(HALVES):
+                for u in halves:
                     nc.tensor.transpose(bank[:, i, u, :], sources[i][:, u * P : (u + 1) * P], ident_f[:])
 
         def copy_words(bank, grouped, pair):
@@ -154,6 +173,12 @@ def tile_singlehead_pa_kernel(tc, q, k_proj, x, Wv, out):
                 out=grouped_words[:, 2 * P * pair : 2 * P * (pair + 1), :].rearrange("p (i m) u -> p i m u", i=2),
                 in_=bank[:].rearrange("p i u m -> p i m u"),
             )
+
+        e_bank_low = psum_e.tile([P, PAIR, HALVES, P], F32)
+
+        def e_bank_zero(step):
+            if step == BEHIND - MT:
+                turn_words(e_bank_low, [words_of(e_all[:, 0, t, :]) for t in range(PAIR)], (1,))
 
         w_grouped = const.tile([P, PASSES * H * PACK], BF16, align_bytes=64)
         w_codes = const.tile([P, PASSES, H], U32, align_bytes=64)
@@ -256,7 +281,7 @@ def tile_singlehead_pa_kernel(tc, q, k_proj, x, Wv, out):
             )
 
         def v_shift(k):
-            if not 0 <= k < QUARTERS or k % BEHIND != BEHIND - 1:
+            if not 0 <= k < QUARTERS or k % SEQUENCE != SEQUENCE - 1:
                 return
             b = (k // 4) // G
             tiles_b = slice(b * MT, (b + 1) * MT)
@@ -274,7 +299,7 @@ def tile_singlehead_pa_kernel(tc, q, k_proj, x, Wv, out):
         neg_local = const.tile([P, B, G, MT], F32)
 
         def local_logits(s):
-            b, rest = (s - LOCAL_BEHIND) // BEHIND, (s - LOCAL_BEHIND) % BEHIND
+            b, rest = (s - LOCAL_BEHIND) // SEQUENCE, (s - LOCAL_BEHIND) % SEQUENCE
             if not (0 <= b < B and rest < LOCAL_STEPS):
                 return
             t = rest // 2
@@ -288,7 +313,7 @@ def tile_singlehead_pa_kernel(tc, q, k_proj, x, Wv, out):
                     )
 
         def local_minimum(s):
-            b, rest = (s - LOCAL_BEHIND) // BEHIND, (s - LOCAL_BEHIND) % BEHIND
+            b, rest = (s - LOCAL_BEHIND) // SEQUENCE, (s - LOCAL_BEHIND) % SEQUENCE
             if not (0 <= b < B and rest == LOCAL_STEPS):
                 return
             nc.vector.memset(neg_logit[0:1, :, b, 0, 0:1], -MASKED)
@@ -312,28 +337,37 @@ def tile_singlehead_pa_kernel(tc, q, k_proj, x, Wv, out):
             if not 0 <= i < TILES or i % MT != 0:
                 return
             qkT = pipe3.tile([P, 2, MT, P], BF16)
-            nc.vector.tensor_copy(out=qkT[:], in_=live["qk_bank", class_of(i)][:])
+            nc.scalar.copy(
+                out=words_of(qkT[:].rearrange("h a t m -> h (a t m)")),
+                in_=words_of(live["qk_bank", class_of(i)][:].rearrange("h a t m -> h (a t m)")),
+            )
             live["qkT", class_of(i)] = qkT
 
         def logits(i):
             if not 0 <= i < TILES:
                 return
-            cls, t = class_of(i), i % MT
+            cls, t = class_of(i), tile_of(i)
             qkT = live["qkT", cls]
             bank = psum_w.tile([P, M], F32, tag="w")
+            first_open = 1 if cls % G == 0 else 0
+            if t > first_open:
+                nc.tensor.matmul(
+                    out=bank[:, first_open * P : t * P], lhsT=qkT[:, 0, t, :],
+                    rhs=qkT[:, 1, first_open:t, :].rearrange("h t m -> h (t m)"), start=True, stop=True,
+                )
             for tk in range(t + 1):
-                block = bank[:, tk * P : (tk + 1) * P]
                 mask = mask_of(cls % G, t, tk)
-                nc.tensor.matmul(out=block, lhsT=qkT[:, 0, t, :], rhs=qkT[:, 1, tk, :], start=True, stop=(mask is None))
                 if mask is not None:
+                    block = bank[:, tk * P : (tk + 1) * P]
+                    nc.tensor.matmul(out=block, lhsT=qkT[:, 0, t, :], rhs=qkT[:, 1, tk, :], start=True, stop=False)
                     nc.tensor.matmul(out=block, lhsT=ident_b[:], rhs=mask[:], start=False, stop=True)
             live["logits", i] = bank
 
         def top(i):
             if not 0 <= i < TILES:
                 return
-            cls, t = class_of(i), i % MT
-            if t == 0:
+            cls, t = class_of(i), tile_of(i)
+            if i % MT == 0:
                 neg_top = small.tile([P, MT], F32)
                 live["neg_top", cls] = neg_top
             keys = (t + 1) * P
@@ -351,8 +385,8 @@ def tile_singlehead_pa_kernel(tc, q, k_proj, x, Wv, out):
         def exponentials(i):
             if not 0 <= i < TILES:
                 return
-            cls, t = class_of(i), i % MT
-            if t == 0:
+            cls, t = class_of(i), tile_of(i)
+            if i % MT == 0:
                 e_sums = small.tile([P, 1 + LW, MT], F32)
                 live["e_sums", cls] = e_sums
             keys = (t // 2 + 1) * 2 * P
@@ -363,29 +397,42 @@ def tile_singlehead_pa_kernel(tc, q, k_proj, x, Wv, out):
             )
 
         def e_turn(i):
-            if not 0 <= i < TILES or i % 2 != 1:
+            if not 0 <= i < TILES or i % PAIR != PAIR - 1:
                 return
-            cls, t = class_of(i), i % MT
-            bank = psum_t.tile([P, 2, HALVES, P], F32, tag="t")
-            turn_words(bank, [words_of(e_all[:, cls % 2, t - 1, :]), words_of(e_all[:, cls % 2, t, :])])
+            cls = class_of(i)
+            rows = [words_of(e_all[:, cls % 2, t, :]) for t in pair_of(i)]
+            if pair_of(i)[0] == 0:
+                bank = e_bank_low
+                turn_words(bank, rows, (0,))
+            else:
+                bank = psum_t.tile([P, PAIR, HALVES, P], F32, tag="t")
+                turn_words(bank, rows)
             live["e_bank", i] = bank
 
         def e_copy(i):
-            if not 0 <= i < TILES or i % 2 != 1:
+            if not 0 <= i < TILES or i % PAIR != PAIR - 1:
                 return
-            cls, t = class_of(i), i % MT
-            if t == 1:
+            cls = class_of(i)
+            if i % MT == PAIR - 1:
                 e_grouped = pipe2.tile([P, M * PACK], BF16, align_bytes=64)
                 live["e_grouped", cls] = e_grouped
-            copy_words(live["e_bank", i], live["e_grouped", cls], t // 2)
+            copy_words(live["e_bank", i], live["e_grouped", cls], pair_of(i)[0] // PAIR)
 
         def e_quantise(i):
-            if not 0 <= i < TILES or i % MT != MT - 1:
+            tiles = piece_of(i)
+            if not tiles:
                 return
-            e_codes = pipe2.tile([P, M], U32, align_bytes=64)
-            e_scales = pipe2.tile([P, M], U8, align_bytes=64)
-            nc.vector.quantize_mx(out=e_codes[:].bitcast(FP8X4), scales=e_scales[:], in_=live["e_grouped", class_of(i)][:])
-            live["e_codes", class_of(i)] = (e_codes, e_scales)
+            cls = class_of(i)
+            if ("e_codes", cls) not in live:
+                e_codes = pipe2.tile([P, M], U32, align_bytes=64)
+                e_scales = pipe2.tile([P, M], U8, align_bytes=64)
+                live["e_codes", cls] = (e_codes, e_scales)
+            e_codes, e_scales = live["e_codes", cls]
+            c0, c1 = tiles[0] * P, (tiles[-1] + 1) * P
+            nc.vector.quantize_mx(
+                out=e_codes[:, c0:c1].bitcast(FP8X4), scales=e_scales[:, c0:c1],
+                in_=live["e_grouped", cls][:, c0 * PACK : c1 * PACK],
+            )
 
         def local_shift(i):
             if not 0 <= i < TILES or i % MT != MT - 1:
@@ -419,23 +466,14 @@ def tile_singlehead_pa_kernel(tc, q, k_proj, x, Wv, out):
             nc.vector.reciprocal(out=inv_den[:], in_=live["den", class_of(i)][:])
             live["inv_den", class_of(i)] = inv_den
 
-        def local_weights(i):
-            if not 0 <= i < TILES or i % MT != MT - 1:
-                return
-            local_w = small.tile([P, LW, MT], F32)
-            nc.vector.tensor_mul(
-                out=local_w[:], in0=live["e_sums", class_of(i)][:, 1:, :],
-                in1=live["inv_den", class_of(i)][:].unsqueeze(1).to_broadcast([P, LW, MT]),
-            )
-            live["local_w", class_of(i)] = local_w
-
         def atrous_product(i):
-            if not 0 <= i < TILES or i % MT != MT - 1:
+            tiles = piece_of(i)
+            if not tiles:
                 return
             cls = class_of(i)
             e_codes, e_scales = live["e_codes", cls]
             atrous = psum_s.tile([P, MT, H], F32, tag="sum")
-            for t in range(MT):
+            for t in tiles:
                 cols = slice(t * P, (t + 1) * P)
                 nc.tensor.matmul_mx(
                     out=atrous[:, t, :],
@@ -443,55 +481,66 @@ def tile_singlehead_pa_kernel(tc, q, k_proj, x, Wv, out):
                     rhs=v_codes[:, cls, :].bitcast(FP8X4), rhs_scale=v_scales[:, cls, :],
                     start=True, stop=True,
                 )
-            live["atrous", cls] = atrous
-
-        def atrous_scaled(i):
-            if not 0 <= i < TILES or i % MT != MT - 1:
-                return
-            cls = class_of(i)
-            part = pipe2.tile([P, MT, H], F32)
-            for t in range(MT):
-                nc.scalar.activation(
-                    out=part[:, t, :], in_=live["atrous", cls][:, t, :], func=ACT.Copy,
-                    scale=live["inv_den", cls][:, t : t + 1],
-                )
-            live["part", cls] = part
+                live["atrous", cls, t] = atrous
 
         def add_local_first(i):
             if not 0 <= i < TILES:
                 return
-            cls, t = class_of(i), i % MT
+            cls, t = class_of(i), tile_of(i)
             b, r = cls // G, cls % G
-            if t == 0:
+            if i % MT == 0:
                 with_one = pipe2.tile([P, MT, H], F32)
                 live["with_one", cls] = with_one
             nc.vector.scalar_tensor_tensor(
                 out=live["with_one", cls][:, t, :], in0=v_ext[:, b * MT + t, LW + r - 1, :],
-                scalar=live["local_w", cls][:, 0, t : t + 1], in1=live["part", cls][:, t, :], op0=ALU.mult, op1=ALU.add,
+                scalar=live["e_sums", cls][:, 1, t : t + 1], in1=live["atrous", cls, t][:, t, :], op0=ALU.mult, op1=ALU.add,
             )
 
         def add_local_second(i):
             if not 0 <= i < TILES:
                 return
-            cls, t = class_of(i), i % MT
+            cls, t = class_of(i), tile_of(i)
             b, r = cls // G, cls % G
-            if t == 0:
-                result = pipe2.tile([P, MT, H], F32)
-                live["result", cls] = result
+            if i % MT == 0:
+                with_two = pipe2.tile([P, MT, H], F32)
+                live["with_two", cls] = with_two
             nc.vector.scalar_tensor_tensor(
-                out=live["result", cls][:, t, :], in0=v_ext[:, b * MT + t, LW + r - 2, :],
-                scalar=live["local_w", cls][:, 1, t : t + 1], in1=live["with_one", cls][:, t, :], op0=ALU.mult, op1=ALU.add,
+                out=live["with_two", cls][:, t, :], in0=v_ext[:, b * MT + t, LW + r - 2, :],
+                scalar=live["e_sums", cls][:, 2, t : t + 1], in1=live["with_one", cls][:, t, :], op0=ALU.mult, op1=ALU.add,
             )
-            if t == MT - 1:
-                nc.sync.dma_start(out=out_tiles[r, :, b * MT : (b + 1) * MT, :], in_=live["result", cls][:])
+
+        def divide(i):
+            if not 0 <= i < TILES:
+                return
+            cls, t = class_of(i), tile_of(i)
+            b, r = cls // G, cls % G
+            if i % MT == 0:
+                result = results.tile([P, MT, H], F32)
+                live["result", cls] = result
+            if i >= TILES - MT:
+                nc.scalar.activation(
+                    out=live["result", cls][:, t, :], in_=live["with_two", cls][:, t, :], func=ACT.Copy,
+                    scale=live["inv_den", cls][:, t : t + 1],
+                )
+            else:
+                nc.gpsimd.tensor_scalar(
+                    out=live["result", cls][:, t, :], in0=live["with_two", cls][:, t, :],
+                    scalar1=live["inv_den", cls][:, t : t + 1], scalar2=1.0, op0=ALU.mult, op1=ALU.mult,
+                )
+            tiles = piece_of(i)
+            if tiles:
+                t0, t1 = tiles[0], tiles[-1] + 1
+                nc.sync.dma_start(out=out_tiles[r, :, b * MT + t0 : b * MT + t1, :], in_=live["result", cls][:, t0:t1, :])
 
         LAST = BEHIND + TILES + 14
         for step in range(LAST):
-            i = step - FRONT_BEHIND
-            j = step - BEHIND
+            i = step - BEHIND
+            local_minimum(step)
             top(i - 1)
-            add_local_first(j - 12)
-            add_local_second(j - 13)
+            add_local_first(i - 11)
+            add_local_second(i - 12)
+            divide(i - 13)
+            e_bank_zero(step)
             w_turn(step)
             x_turn(step)
             w_copy(step - 1)
@@ -499,23 +548,20 @@ def tile_singlehead_pa_kernel(tc, q, k_proj, x, Wv, out):
             w_quantise(step - 2)
             x_quantise(step - 2)
             v_project(step - 3)
-            atrous_product(j - 7)
+            atrous_product(i - 7)
             v_copy_rows(step - 4)
             v_copy_keys(step - 4)
             v_quantise(step - 5)
             v_shift(step - 5)
             local_logits(step)
-            local_minimum(step)
-            qk_turn(i + 5)
-            qk_copy(i + 4)
+            qk_turn(i + 4)
+            qk_copy(i + 3)
             logits(i)
             exponentials(i - 2)
             e_turn(i - 3)
             e_copy(i - 4)
             e_quantise(i - 5)
-            atrous_scaled(j - 8)
             local_shift(i - 2)
             local_exp(i - 3)
             denominator(i - 4)
             inverse(i - 5)
-            local_weights(i - 6)

@@ -68,7 +68,7 @@ def words_of(tile_2d):
 def tile_singlehead_pa_kernel(tc, q, k_proj, x, Wv, out):
     nc = tc.nc
     with ExitStack() as stack:
-        stack.enter_context(tc.manual_schedule())
+        stack.enter_context(tc.manual_schedule(engines={mybir.EngineType.SP}))
         const = stack.enter_context(tc.tile_pool(name="const", bufs=1))
         x_pool = stack.enter_context(tc.tile_pool(name="x", bufs=NC))
         pipe2 = stack.enter_context(tc.tile_pool(name="pipe2", bufs=2))
@@ -533,7 +533,7 @@ def tile_singlehead_pa_kernel(tc, q, k_proj, x, Wv, out):
                 nc.sync.dma_start(out=out_tiles[r, :, b * MT + t0 : b * MT + t1, :], in_=live["result", cls][:, t0:t1, :])
 
         LAST = BEHIND + TILES + 14
-        for step in range(LAST):
+        def run_step(step):
             i = step - BEHIND
             local_minimum(step)
             top(i - 1)
@@ -565,3 +565,9 @@ def tile_singlehead_pa_kernel(tc, q, k_proj, x, Wv, out):
             local_exp(i - 3)
             denominator(i - 4)
             inverse(i - 5)
+
+        with tc.manual_schedule():
+            for step in range(BEHIND):
+                run_step(step)
+        for step in range(BEHIND, LAST):
+            run_step(step)

@@ -68,7 +68,9 @@ def words_of(tile_2d):
 def tile_singlehead_pa_kernel(tc, q, k_proj, x, Wv, out):
     nc = tc.nc
     with ExitStack() as stack:
-        stack.enter_context(tc.manual_schedule(engines={mybir.EngineType.SP}))
+        stack.enter_context(tc.manual_schedule(engines={
+            mybir.EngineType.PE, mybir.EngineType.Activation, mybir.EngineType.Pool, mybir.EngineType.SP
+        }))
         const = stack.enter_context(tc.tile_pool(name="const", bufs=1))
         x_pool = stack.enter_context(tc.tile_pool(name="x", bufs=NC))
         pipe2 = stack.enter_context(tc.tile_pool(name="pipe2", bufs=2))
@@ -540,6 +542,7 @@ def tile_singlehead_pa_kernel(tc, q, k_proj, x, Wv, out):
             add_local_first(i - 11)
             add_local_second(i - 12)
             divide(i - 13)
+            logits(i)
             e_bank_zero(step)
             w_turn(step)
             x_turn(step)
@@ -556,7 +559,6 @@ def tile_singlehead_pa_kernel(tc, q, k_proj, x, Wv, out):
             local_logits(step)
             qk_turn(i + 4)
             qk_copy(i + 3)
-            logits(i)
             exponentials(i - 2)
             e_turn(i - 3)
             e_copy(i - 4)

@@ -34,6 +34,7 @@ QUARTERS = NC * 4
 TILES = NC * MT
 SEQUENCE = G * MT
 BEHIND = SEQUENCE - MT
+FRONT_BEHIND = BEHIND - 2
 LOCAL_BEHIND = 5
 LOCAL_STEPS = 2 * MT
 
@@ -76,7 +77,7 @@ def tile_singlehead_pa_kernel(tc, q, k_proj, x, Wv, out):
         pipe2 = stack.enter_context(tc.tile_pool(name="pipe2", bufs=2))
         pipe3 = stack.enter_context(tc.tile_pool(name="pipe3", bufs=3))
         results = stack.enter_context(tc.tile_pool(name="results", bufs=NC))
-        small = stack.enter_context(tc.tile_pool(name="small", bufs=6))
+        small = stack.enter_context(tc.tile_pool(name="small", bufs=8))
         psum_w = stack.enter_context(tc.psum_pool(name="psum_w", bufs=4))
         psum_e = stack.enter_context(tc.psum_pool(name="psum_e", bufs=1))
         psum_t = stack.enter_context(tc.psum_pool(name="psum_t", bufs=1))
@@ -117,9 +118,9 @@ def tile_singlehead_pa_kernel(tc, q, k_proj, x, Wv, out):
             return causal if tk == t else None
 
         e_all = const.tile([P, 2, MT, M], BF16)
-        nc.vector.memset(e_all[:, :, 0:PAIR, M // 2 :], 0.0)
+        nc.vector.memset(e_all[:, :, 0:PAIR, :], 0.0)
         neg_even = {}
-        for t in range(0, MT, 2):
+        for t in range(PAIR, MT, PAIR):
             for i in range(2):
                 neg_tile = const.tile([P, (t + 2) * P], F32, name="neg_even_%d_%d" % (t, i))
                 nc.gpsimd.memset(neg_tile[:, (t + 1) * P :], -MASKED)
@@ -134,22 +135,22 @@ def tile_singlehead_pa_kernel(tc, q, k_proj, x, Wv, out):
         first = k_rows[LW : LW + (P - 1) * G, :].rearrange("(m f) h -> m f h", f=G)
         nc.vector.memset(k_ext[0:1, 0, 0:LW, :], 0.0)
 
-        def load_q_k(b):
-            tiles_b = slice(b * MT, (b + 1) * MT)
+        def load_q_k(b, t0, t1):
+            tiles_b = slice(b * MT + t0, b * MT + t1)
             nc.sync.dma_start(out=q_sb[:, tiles_b, :, :], in_=q_tiles[:, tiles_b, :, :])
             nc.sync.dma_start(out=k_ext[:, tiles_b, LW:, :], in_=k_tiles[:, tiles_b, :, :])
-            if b == 0:
+            if b == 0 and t0 == 0:
                 nc.sync.dma_start(out=k_ext[1 : P - 1, 0, 0:LW, :], in_=first[: P - 2, 0:LW, :])
                 nc.sync.dma_start(out=k_ext[P - 1 : P, 0, 0:LW, :], in_=first[P - 2 :, 0:LW, :])
-            after_first = slice(max(b * MT, 1), (b + 1) * MT)
+            after_first = slice(max(tiles_b.start, 1), tiles_b.stop)
             nc.sync.dma_start(
-                out=k_ext[:, after_first, 0:LW, :], in_=early[:, max(b * MT, 1) - 1 : (b + 1) * MT - 1, 0:LW, :]
+                out=k_ext[:, after_first, 0:LW, :], in_=early[:, after_first.start - 1 : after_first.stop - 1, 0:LW, :]
             )
 
         x_sb = []
         for cls in range(NC):
             x_class = x_pool.tile([P, MT * D], BF16, tag="x")
-            pieces = 2 if cls == 0 else 1
+            pieces = 2 if cls in (0, 2, 3) else 1
             for piece in range(pieces):
                 t0, t1 = piece * MT // pieces, (piece + 1) * MT // pieces
                 nc.sync.dma_start(
@@ -160,9 +161,10 @@ def tile_singlehead_pa_kernel(tc, q, k_proj, x, Wv, out):
                     nc.sync.dma_start(out=wv_sb[:], in_=Wv)
             x_sb.append(x_class)
             if cls == 1:
-                load_q_k(0)
+                load_q_k(0, 0, PAIR)
+                load_q_k(0, PAIR, MT)
             if cls == G:
-                load_q_k(1)
+                load_q_k(1, 0, MT)
 
         def turn_words(bank, sources, halves=range(HALVES)):
             for i in range(2):
@@ -179,7 +181,7 @@ def tile_singlehead_pa_kernel(tc, q, k_proj, x, Wv, out):
         e_bank_low = psum_e.tile([P, PAIR, HALVES, P], F32)
 
         def e_bank_zero(step):
-            if step == BEHIND - MT:
+            if step == FRONT_BEHIND - MT:
                 turn_words(e_bank_low, [words_of(e_all[:, 0, t, :]) for t in range(PAIR)], (1,))
 
         w_grouped = const.tile([P, PASSES * H * PACK], BF16, align_bytes=64)
@@ -316,12 +318,15 @@ def tile_singlehead_pa_kernel(tc, q, k_proj, x, Wv, out):
 
         def local_minimum(s):
             b, rest = (s - LOCAL_BEHIND) // SEQUENCE, (s - LOCAL_BEHIND) % SEQUENCE
-            if not (0 <= b < B and rest == LOCAL_STEPS):
+            if not (0 <= b < B and 0 < rest <= LOCAL_STEPS and rest % 2 == 0):
                 return
-            nc.vector.memset(neg_logit[0:1, :, b, 0, 0:1], -MASKED)
-            nc.vector.memset(neg_logit[0:1, 1, b, 1, 0:1], -MASKED)
+            t = rest // 2 - 1
+            if t == 0:
+                nc.vector.memset(neg_logit[0:1, :, b, 0, 0:1], -MASKED)
+                nc.vector.memset(neg_logit[0:1, 1, b, 1, 0:1], -MASKED)
             nc.vector.tensor_tensor(
-                out=neg_local[:, b, :, :], in0=neg_logit[:, 0, b, :, :], in1=neg_logit[:, 1, b, :, :], op=ALU.min
+                out=neg_local[:, b, :, t : t + 1],
+                in0=neg_logit[:, 0, b, :, t : t + 1], in1=neg_logit[:, 1, b, :, t : t + 1], op=ALU.min,
             )
 
         def qk_turn(i):
@@ -330,7 +335,7 @@ def tile_singlehead_pa_kernel(tc, q, k_proj, x, Wv, out):
             b, r = class_of(i) // G, class_of(i) % G
             qk_bank = psum_t.tile([P, 2, MT, P], BF16, tag="t")
             for t in range(MT):
-                nc.tensor.transpose(qk_bank[:, 0, t, :], q_sb[:, b * MT + t, r, :], ident_b[:])
+                nc.tensor.matmul(out=qk_bank[:, 0, t, :], lhsT=q_sb[:, b * MT + t, r, :], rhs=ident_b[:], start=True, stop=True)
             for t in range(MT):
                 nc.tensor.transpose(qk_bank[:, 1, t, :], k_ext[:, b * MT + t, LW + r, :], ident_b[:])
             live["qk_bank", class_of(i)] = qk_bank
@@ -373,7 +378,7 @@ def tile_singlehead_pa_kernel(tc, q, k_proj, x, Wv, out):
                 neg_top = small.tile([P, MT], F32)
                 live["neg_top", cls] = neg_top
             keys = (t + 1) * P
-            if t % 2 == 0:
+            if (t, cls % 2) in neg_even:
                 neg_scaled = neg_even[t, cls % 2]
             else:
                 neg_scaled = pipe3.tile([P, M], F32)
@@ -392,9 +397,13 @@ def tile_singlehead_pa_kernel(tc, q, k_proj, x, Wv, out):
                 e_sums = small.tile([P, 1 + LW, MT], F32)
                 live["e_sums", cls] = e_sums
             keys = (t // 2 + 1) * 2 * P
+            e_rows = e_all[:, cls % 2, t, :keys].rearrange("p (u m e) -> p u m e", e=2, m=P)
+            if t == 0:
+                e_rows, source = e_rows[:, 0, :, 0], live["neg_scaled", i][:, :P]
+            else:
+                source = live["neg_scaled", i][:, :keys].rearrange("p (u e m) -> p u m e", e=2, m=P)
             nc.scalar.activation(
-                out=e_all[:, cls % 2, t, :keys].rearrange("p (u m e) -> p u m e", e=2, m=P),
-                in_=live["neg_scaled", i][:, :keys].rearrange("p (u e m) -> p u m e", e=2, m=P), func=ACT.Exp,
+                out=e_rows, in_=source, func=ACT.Exp,
                 bias=live["neg_top", cls][:, t : t + 1], scale=-1.0, accum_out=live["e_sums", cls][:, 0, t : t + 1],
             )
 
@@ -426,8 +435,8 @@ def tile_singlehead_pa_kernel(tc, q, k_proj, x, Wv, out):
                 return
             cls = class_of(i)
             if ("e_codes", cls) not in live:
-                e_codes = pipe2.tile([P, M], U32, align_bytes=64)
-                e_scales = pipe2.tile([P, M], U8, align_bytes=64)
+                e_codes = pipe3.tile([P, M], U32, align_bytes=64)
+                e_scales = pipe3.tile([P, M], U8, align_bytes=64)
                 live["e_codes", cls] = (e_codes, e_scales)
             e_codes, e_scales = live["e_codes", cls]
             c0, c1 = tiles[0] * P, (tiles[-1] + 1) * P
@@ -536,12 +545,14 @@ def tile_singlehead_pa_kernel(tc, q, k_proj, x, Wv, out):
 
         LAST = BEHIND + TILES + 14
         def run_step(step):
-            i = step - BEHIND
+            i = step - FRONT_BEHIND
+            j = step - BEHIND
+            v_shift(step - 5)
             local_minimum(step)
             top(i - 1)
-            add_local_first(i - 11)
-            add_local_second(i - 12)
-            divide(i - 13)
+            add_local_first(j - 11)
+            add_local_second(j - 12)
+            divide(j - 13)
             logits(i)
             e_bank_zero(step)
             w_turn(step)
@@ -551,11 +562,10 @@ def tile_singlehead_pa_kernel(tc, q, k_proj, x, Wv, out):
             w_quantise(step - 2)
             x_quantise(step - 2)
             v_project(step - 3)
-            atrous_product(i - 7)
+            atrous_product(j - 7)
             v_copy_rows(step - 4)
             v_copy_keys(step - 4)
             v_quantise(step - 5)
-            v_shift(step - 5)
             local_logits(step)
             qk_turn(i + 4)
             qk_copy(i + 3)
@@ -569,7 +579,7 @@ def tile_singlehead_pa_kernel(tc, q, k_proj, x, Wv, out):
             inverse(i - 5)
 
         with tc.manual_schedule():
-            for step in range(BEHIND):
+            for step in range(FRONT_BEHIND):
                 run_step(step)
-        for step in range(BEHIND, LAST):
+        for step in range(FRONT_BEHIND, LAST):
             run_step(step)

@@ -34,7 +34,7 @@ QUARTERS = NC * 4
 TILES = NC * MT
 SEQUENCE = G * MT
 BEHIND = SEQUENCE - MT
-FRONT_BEHIND = BEHIND - 2
+FRONT_BEHIND = BEHIND - 1
 LOCAL_BEHIND = 5
 LOCAL_STEPS = 2 * MT
 
@@ -528,7 +528,7 @@ def tile_singlehead_pa_kernel(tc, q, k_proj, x, Wv, out):
             if i % MT == 0:
                 result = results.tile([P, MT, H], F32)
                 live["result", cls] = result
-            if i >= TILES - MT:
+            if i >= TILES - 2 * MT:
                 nc.scalar.activation(
                     out=live["result", cls][:, t, :], in_=live["with_two", cls][:, t, :], func=ACT.Copy,
                     scale=live["inv_den", cls][:, t : t + 1],

from contextlib import ExitStack

import concourse.mybir as mybir
from concourse.masks import make_identity

F32 = mybir.dt.float32
BF16 = mybir.dt.bfloat16
U32 = mybir.dt.uint32
U8 = mybir.dt.uint8
FP8X4 = mybir.dt.float8_e4m3fn_x4
ALU = mybir.AluOpType
ACT = mybir.ActivationFunctionType
AX = mybir.AxisListType

B, S, D, H = 2, 2048, 1024, 128
G = 4
LW = 2
M = S // G
P = 128
MT = M // P
NT = B * MT
NC = B * G
TILE_TOKENS = P * G
PACK = 4
K_PASS = P * PACK
PASSES = D // K_PASS
HALVES = 2
PAIR = 2
WORDS = K_PASS // 2
SCALE = 1.0 / 32.0
MASKED = -1.0e30

QUARTERS = NC * 4
TILES = NC * MT
SEQUENCE = G * MT
BEHIND = SEQUENCE - MT
FRONT_BEHIND = BEHIND - 1
LOCAL_BEHIND = 5
LOCAL_STEPS = 2 * MT

FLOPS = 2 * B * S * D * H + 2 * (2 * B * G * M * M * H)


def class_of(i):
    return i // MT // G * G + (i // MT + LW) % G


def tile_of(i):
    return i % MT


def pair_of(i):
    t = tile_of(i) // PAIR * PAIR
    return [t, t + 1]


def piece_of(i):
    if not 0 <= i < TILES:
        return []
    if i >= TILES - MT:
        return pair_of(i) if i % PAIR == PAIR - 1 else []
    return list(range(MT)) if i % MT == MT - 1 else []


def words_of(tile_2d):
    return tile_2d.bitcast(F32)


def tile_singlehead_pa_kernel(tc, q, k_proj, x, Wv, out):
    nc = tc.nc
    with ExitStack() as stack:
        stack.enter_context(tc.manual_schedule(engines={
            mybir.EngineType.PE, mybir.EngineType.Activation, mybir.EngineType.Pool, mybir.EngineType.SP
        }))
        const = stack.enter_context(tc.tile_pool(name="const", bufs=1))
        x_pool = stack.enter_context(tc.tile_pool(name="x", bufs=NC))
        pipe2 = stack.enter_context(tc.tile_pool(name="pipe2", bufs=2))
        pipe3 = stack.enter_context(tc.tile_pool(name="pipe3", bufs=3))
        results = stack.enter_context(tc.tile_pool(name="results", bufs=NC))
        small = stack.enter_context(tc.tile_pool(name="small", bufs=8))
        psum_w = stack.enter_context(tc.psum_pool(name="psum_w", bufs=4))
        psum_e = stack.enter_context(tc.psum_pool(name="psum_e", bufs=1))
        psum_t = stack.enter_context(tc.psum_pool(name="psum_t", bufs=1))
        psum_s = stack.enter_context(tc.psum_pool(name="psum_s", bufs=2))

        q_tiles = q.flatten_outer_dims().rearrange("(T m r) h -> m T r h", T=NT, m=P, r=G)
        k_rows = k_proj.flatten_outer_dims()
        k_tiles = k_rows.rearrange("(T m r) h -> m T r h", T=NT, m=P, r=G)
        x_tiles = x.flatten_outer_dims().rearrange("(T m r) k -> r m T k", T=NT, m=P, r=G)
        out_tiles = out.flatten_outer_dims().rearrange("(T m r) h -> r m T h", T=NT, m=P, r=G)

        ident_f = const.tile([P, P], F32)
        make_identity(nc, ident_f[:])
        ident_b = const.tile([P, P], BF16)
        make_identity(nc, ident_b[:])
        causal_f = const.tile([P, P], F32)
        nc.gpsimd.memset(causal_f[:], 0.0)
        nc.gpsimd.affine_select(
            out=causal_f[:], in_=causal_f[:], pattern=[[-1, P]], compare_op=ALU.is_ge,
            fill=MASKED, base=0, channel_multiplier=1,
        )
        causal_key0_f = const.tile([P, P], F32)
        nc.gpsimd.affine_select(
            out=causal_key0_f[:], in_=causal_f[:], pattern=[[P, P]], compare_op=ALU.is_ge,
            fill=MASKED, base=0, channel_multiplier=-1,
        )
        causal = const.tile([P, P], BF16)
        nc.vector.tensor_copy(out=causal[:], in_=causal_f[:])
        causal_key0 = const.tile([P, P], BF16)
        nc.vector.tensor_copy(out=causal_key0[:], in_=causal_key0_f[:])
        key0 = const.tile([P, P], BF16)
        nc.vector.memset(key0[:], 0.0)
        nc.vector.memset(key0[:, 0:1], MASKED)

        def mask_of(r, t, tk):
            if r == 0 and tk == 0:
                return causal_key0 if t == 0 else key0
            return causal if tk == t else None

        e_all = const.tile([P, 2, MT, M], BF16)
        nc.vector.memset(e_all[:, :, 0:PAIR, :], 0.0)
        neg_even = {}
        for t in range(PAIR, MT, PAIR):
            for i in range(2):
                neg_tile = const.tile([P, (t + 2) * P], F32, name="neg_even_%d_%d" % (t, i))
                nc.gpsimd.memset(neg_tile[:, (t + 1) * P :], -MASKED)
                neg_even[t, i] = neg_tile

        wv_sb = const.tile([P, D], BF16)
        q_sb = const.tile([P, NT, G, H], BF16)
        k_ext = const.tile([P, NT, LW + G, H], BF16)
        early = k_rows[TILE_TOKENS - LW : TILE_TOKENS - LW + (NT - 1) * TILE_TOKENS, :].rearrange(
            "(T m f) h -> m T f h", T=NT - 1, m=P, f=G
        )
        first = k_rows[LW : LW + (P - 1) * G, :].rearrange("(m f) h -> m f h", f=G)
        nc.vector.memset(k_ext[0:1, 0, 0:LW, :], 0.0)

        def load_q_k(b, t0, t1):
            tiles_b = slice(b * MT + t0, b * MT + t1)
            nc.sync.dma_start(out=q_sb[:, tiles_b, :, :], in_=q_tiles[:, tiles_b, :, :])
            nc.sync.dma_start(out=k_ext[:, tiles_b, LW:, :], in_=k_tiles[:, tiles_b, :, :])
            if b == 0 and t0 == 0:
                nc.sync.dma_start(out=k_ext[1 : P - 1, 0, 0:LW, :], in_=first[: P - 2, 0:LW, :])
                nc.sync.dma_start(out=k_ext[P - 1 : P, 0, 0:LW, :], in_=first[P - 2 :, 0:LW, :])
            after_first = slice(max(tiles_b.start, 1), tiles_b.stop)
            nc.sync.dma_start(
                out=k_ext[:, after_first, 0:LW, :], in_=early[:, after_first.start - 1 : after_first.stop - 1, 0:LW, :]
            )

        x_sb = []
        for cls in range(NC):
            x_class = x_pool.tile([P, MT * D], BF16, tag="x")
            pieces = 2 if cls in (0, 2, 3) else 1
            for piece in range(pieces):
                t0, t1 = piece * MT // pieces, (piece + 1) * MT // pieces
                nc.sync.dma_start(
                    out=x_class[:, t0 * D : t1 * D].rearrange("p (t k) -> p t k", t=t1 - t0),
                    in_=x_tiles[cls % G, :, (cls // G) * MT + t0 : (cls // G) * MT + t1, :],
                )
                if cls == 0 and piece == 0:
                    nc.sync.dma_start(out=wv_sb[:], in_=Wv)
            x_sb.append(x_class)
            if cls == 1:
                load_q_k(0, 0, PAIR)
                load_q_k(0, PAIR, MT)
            if cls == G:
                load_q_k(1, 0, MT)

        def turn_words(bank, sources, halves=range(HALVES)):
            for i in range(2):
                for u in halves:
                    nc.tensor.transpose(bank[:, i, u, :], sources[i][:, u * P : (u + 1) * P], ident_f[:])

        def copy_words(bank, grouped, pair):
            grouped_words = words_of(grouped[:]).rearrange("p (c u) -> p c u", u=HALVES)
            nc.scalar.copy(
                out=grouped_words[:, 2 * P * pair : 2 * P * (pair + 1), :].rearrange("p (i m) u -> p i m u", i=2),
                in_=bank[:].rearrange("p i u m -> p i m u"),
            )

        e_bank_low = psum_e.tile([P, PAIR, HALVES, P], F32)

        def e_bank_zero(step):
            if step == FRONT_BEHIND - MT:
                turn_words(e_bank_low, [words_of(e_all[:, 0, t, :]) for t in range(PAIR)], (1,))

        w_grouped = const.tile([P, PASSES * H * PACK], BF16, align_bytes=64)
        w_codes = const.tile([P, PASSES, H], U32, align_bytes=64)
        w_scales = const.tile([P, PASSES, H], U8, align_bytes=64)

        def w_turn(k):
            if k != 1:
                return
            w_bank = psum_w.tile([P, PASSES, HALVES, H], F32, tag="w")
            wv_words = words_of(wv_sb[:])
            turn_words(w_bank, [wv_words[:, g * WORDS : (g + 1) * WORDS] for g in range(PASSES)])
            live["w_bank"] = w_bank

        def w_copy(k):
            if k == 1:
                copy_words(live["w_bank"], w_grouped, 0)

        def w_quantise(k):
            if k == 1:
                nc.vector.quantize_mx(
                    out=w_codes[:].rearrange("p g h -> p (g h)").bitcast(FP8X4),
                    scales=w_scales[:].rearrange("p g h -> p (g h)"),
                    in_=w_grouped[:],
                )

        live = {}

        def x_turn(k):
            if not 0 <= k < QUARTERS:
                return
            cls, pair, g = k // 4, (k % 4) // 2, k % 2
            x_words = words_of(x_sb[cls][:])
            starts = [(2 * pair + i) * (D // 2) + g * WORDS for i in range(2)]
            bank = psum_w.tile([P, PAIR, HALVES, P], F32, tag="w")
            turn_words(bank, [x_words[:, w0 : w0 + WORDS] for w0 in starts])
            live["x_bank", k] = bank

        def x_copy(k):
            if not 0 <= k < QUARTERS:
                return
            if k % 2 == 0:
                x_grouped = pipe3.tile([P, PASSES * PAIR * P * PACK], BF16, align_bytes=64)
                live["x_grouped", k // 2] = x_grouped
            copy_words(live["x_bank", k], live["x_grouped", k // 2], k % 2)

        def x_quantise(k):
            if not 0 <= k < QUARTERS or k % 2 != 1:
                return
            cls, pair = k // 4, (k % 4) // 2
            if pair == 0:
                x_codes = pipe2.tile([P, MT // PAIR, PASSES * PAIR * P], U32, align_bytes=64)
                x_scales = pipe2.tile([P, MT // PAIR, PASSES * PAIR * P], U8, align_bytes=64)
                live["x_codes", cls] = (x_codes, x_scales)
            codes, scales = live["x_codes", cls]
            nc.vector.quantize_mx(
                out=codes[:, pair, :].bitcast(FP8X4), scales=scales[:, pair, :], in_=live["x_grouped", k // 2][:]
            )

        def v_project(k):
            if not 0 <= k < QUARTERS or k % 4 != 3:
                return
            codes, scales = live["x_codes", k // 4]
            v_sum = psum_s.tile([P, MT, H], F32, tag="sum")
            for t in range(MT):
                for g in range(PASSES):
                    c0 = (g * PAIR + t % PAIR) * P
                    nc.tensor.matmul_mx(
                        out=v_sum[:, t, :],
                        lhsT=codes[:, t // PAIR, c0 : c0 + P].bitcast(FP8X4), lhsT_scale=scales[:, t // PAIR, c0 : c0 + P],
                        rhs=w_codes[:, g, :].bitcast(FP8X4), rhs_scale=w_scales[:, g, :],
                        start=(g == 0), stop=(g == PASSES - 1),
                    )
            live["v_sum", k // 4] = v_sum

        v_ext = const.tile([P, NT, LW + G, H], F32)
        for b in range(B):
            nc.vector.memset(v_ext[0:1, b * MT, 0:LW, :], 0.0)
        v_codes = const.tile([P, NC, H], U32, align_bytes=64)
        v_scales = const.tile([P, NC, H], U8, align_bytes=64)

        def v_copy_rows(k):
            if not 0 <= k < QUARTERS or k % 4 != 3:
                return
            b, r = (k // 4) // G, (k // 4) % G
            nc.scalar.copy(out=v_ext[:, b * MT : (b + 1) * MT, LW + r, :], in_=live["v_sum", k // 4][:])

        def v_copy_keys(k):
            if not 0 <= k < QUARTERS or k % 4 != 3:
                return
            v_grouped = pipe2.tile([P, H, PACK], BF16, align_bytes=64)
            nc.scalar.copy(out=v_grouped[:], in_=live["v_sum", k // 4][:].rearrange("p j h -> p h j"))
            live["v_grouped", k // 4] = v_grouped

        def v_quantise(k):
            if not 0 <= k < QUARTERS or k % 4 != 3:
                return
            nc.vector.quantize_mx(
                out=v_codes[:, k // 4, :].bitcast(FP8X4), scales=v_scales[:, k // 4, :],
                in_=live["v_grouped", k // 4][:].rearrange("p h j -> p (h j)"),
            )

        def v_shift(k):
            if not 0 <= k < QUARTERS or k % SEQUENCE != SEQUENCE - 1:
                return
            b = (k // 4) // G
            tiles_b = slice(b * MT, (b + 1) * MT)
            half = P // 2
            for src, dst, n in ((0, 1, half), (half, half + 1, half - 1)):
                nc.sync.dma_start(
                    out=v_ext[dst : dst + n, tiles_b, 0:LW, :], in_=v_ext[src : src + n, tiles_b, G : G + LW, :]
                )
            nc.sync.dma_start(
                out=v_ext[0:1, b * MT + 1 : (b + 1) * MT, 0:LW, :],
                in_=v_ext[P - 1 : P, b * MT : (b + 1) * MT - 1, G : G + LW, :],
            )

        neg_logit = const.tile([P, LW, B, G, MT], F32)
        neg_local = const.tile([P, B, G, MT], F32)

        def local_logits(s):
            b, rest = (s - LOCAL_BEHIND) // SEQUENCE, (s - LOCAL_BEHIND) % SEQUENCE
            if not (0 <= b < B and rest < LOCAL_STEPS):
                return
            t = rest // 2
            T = b * MT + t
            for r in (2 * (rest % 2), 2 * (rest % 2) + 1):
                for d in range(1, LW + 1):
                    product = pipe2.tile([P, H], F32)
                    nc.vector.scalar_tensor_tensor(
                        out=product[:], in0=q_sb[:, T, r, :], scalar=-SCALE, in1=k_ext[:, T, LW + r - d, :],
                        op0=ALU.mult, op1=ALU.mult, accum_out=neg_logit[:, d - 1, b, r, t : t + 1],
                    )

        def local_minimum(s):
            b, rest = (s - LOCAL_BEHIND) // SEQUENCE, (s - LOCAL_BEHIND) % SEQUENCE
            if not (0 <= b < B and 0 < rest <= LOCAL_STEPS and rest % 2 == 0):
                return
            t = rest // 2 - 1
            if t == 0:
                nc.vector.memset(neg_logit[0:1, :, b, 0, 0:1], -MASKED)
                nc.vector.memset(neg_logit[0:1, 1, b, 1, 0:1], -MASKED)
            nc.vector.tensor_tensor(
                out=neg_local[:, b, :, t : t + 1],
                in0=neg_logit[:, 0, b, :, t : t + 1], in1=neg_logit[:, 1, b, :, t : t + 1], op=ALU.min,
            )

        def qk_turn(i):
            if not 0 <= i < TILES or i % MT != 0:
                return
            b, r = class_of(i) // G, class_of(i) % G
            qk_bank = psum_t.tile([P, 2, MT, P], BF16, tag="t")
            for t in range(MT):
                nc.tensor.matmul(out=qk_bank[:, 0, t, :], lhsT=q_sb[:, b * MT + t, r, :], rhs=ident_b[:], start=True, stop=True)
            for t in range(MT):
                nc.tensor.transpose(qk_bank[:, 1, t, :], k_ext[:, b * MT + t, LW + r, :], ident_b[:])
            live["qk_bank", class_of(i)] = qk_bank

        def qk_copy(i):
            if not 0 <= i < TILES or i % MT != 0:
                return
            qkT = pipe3.tile([P, 2, MT, P], BF16)
            nc.scalar.copy(
                out=words_of(qkT[:].rearrange("h a t m -> h (a t m)")),
                in_=words_of(live["qk_bank", class_of(i)][:].rearrange("h a t m -> h (a t m)")),
            )
            live["qkT", class_of(i)] = qkT

        def logits(i):
            if not 0 <= i < TILES:
                return
            cls, t = class_of(i), tile_of(i)
            qkT = live["qkT", cls]
            bank = psum_w.tile([P, M], F32, tag="w")
            first_open = 1 if cls % G == 0 else 0
            if t > first_open:
                nc.tensor.matmul(
                    out=bank[:, first_open * P : t * P], lhsT=qkT[:, 0, t, :],
                    rhs=qkT[:, 1, first_open:t, :].rearrange("h t m -> h (t m)"), start=True, stop=True,
                )
            for tk in range(t + 1):
                mask = mask_of(cls % G, t, tk)
                if mask is not None:
                    block = bank[:, tk * P : (tk + 1) * P]
                    nc.tensor.matmul(out=block, lhsT=qkT[:, 0, t, :], rhs=qkT[:, 1, tk, :], start=True, stop=False)
                    nc.tensor.matmul(out=block, lhsT=ident_b[:], rhs=mask[:], start=False, stop=True)
            live["logits", i] = bank

        def top(i):
            if not 0 <= i < TILES:
                return
            cls, t = class_of(i), tile_of(i)
            if i % MT == 0:
                neg_top = small.tile([P, MT], F32)
                live["neg_top", cls] = neg_top
            keys = (t + 1) * P
            if (t, cls % 2) in neg_even:
                neg_scaled = neg_even[t, cls % 2]
            else:
                neg_scaled = pipe3.tile([P, M], F32)
            nc.vector.tensor_scalar(
                out=neg_scaled[:, :keys], in0=live["logits", i][:, :keys], scalar1=-SCALE,
                scalar2=neg_local[:, cls // G, cls % G, t : t + 1], op0=ALU.mult, op1=ALU.min,
                accum_out=live["neg_top", cls][:, t : t + 1],
            )
            live["neg_scaled", i] = neg_scaled

        def exponentials(i):
            if not 0 <= i < TILES:
                return
            cls, t = class_of(i), tile_of(i)
            if i % MT == 0:
                e_sums = small.tile([P, 1 + LW, MT], F32)
                live["e_sums", cls] = e_sums
            keys = (t // 2 + 1) * 2 * P
            e_rows = e_all[:, cls % 2, t, :keys].rearrange("p (u m e) -> p u m e", e=2, m=P)
            if t == 0:
                e_rows, source = e_rows[:, 0, :, 0], live["neg_scaled", i][:, :P]
            else:
                source = live["neg_scaled", i][:, :keys].rearrange("p (u e m) -> p u m e", e=2, m=P)
            nc.scalar.activation(
                out=e_rows, in_=source, func=ACT.Exp,
                bias=live["neg_top", cls][:, t : t + 1], scale=-1.0, accum_out=live["e_sums", cls][:, 0, t : t + 1],
            )

        def e_turn(i):
            if not 0 <= i < TILES or i % PAIR != PAIR - 1:
                return
            cls = class_of(i)
            rows = [words_of(e_all[:, cls % 2, t, :]) for t in pair_of(i)]
            if pair_of(i)[0] == 0:
                bank = e_bank_low
                turn_words(bank, rows, (0,))
            else:
                bank = psum_t.tile([P, PAIR, HALVES, P], F32, tag="t")
                turn_words(bank, rows)
            live["e_bank", i] = bank

        def e_copy(i):
            if not 0 <= i < TILES or i % PAIR != PAIR - 1:
                return
            cls = class_of(i)
            if i % MT == PAIR - 1:
                e_grouped = pipe2.tile([P, M * PACK], BF16, align_bytes=64)
                live["e_grouped", cls] = e_grouped
            copy_words(live["e_bank", i], live["e_grouped", cls], pair_of(i)[0] // PAIR)

        def e_quantise(i):
            tiles = piece_of(i)
            if not tiles:
                return
            cls = class_of(i)
            if ("e_codes", cls) not in live:
                e_codes = pipe3.tile([P, M], U32, align_bytes=64)
                e_scales = pipe3.tile([P, M], U8, align_bytes=64)
                live["e_codes", cls] = (e_codes, e_scales)
            e_codes, e_scales = live["e_codes", cls]
            c0, c1 = tiles[0] * P, (tiles[-1] + 1) * P
            nc.vector.quantize_mx(
                out=e_codes[:, c0:c1].bitcast(FP8X4), scales=e_scales[:, c0:c1],
                in_=live["e_grouped", cls][:, c0 * PACK : c1 * PACK],
            )

        def local_shift(i):
            if not 0 <= i < TILES or i % MT != MT - 1:
                return
            cls = class_of(i)
            shifted = small.tile([P, LW, MT], F32)
            nc.vector.tensor_sub(
                out=shifted[:], in0=live["neg_top", cls][:].unsqueeze(1).to_broadcast([P, LW, MT]),
                in1=neg_logit[:, :, cls // G, cls % G, :],
            )
            live["shifted", cls] = shifted

        def local_exp(i):
            if not 0 <= i < TILES or i % MT != MT - 1:
                return
            nc.scalar.activation(
                out=live["e_sums", class_of(i)][:, 1:, :], in_=live["shifted", class_of(i)][:], func=ACT.Exp
            )

        def denominator(i):
            if not 0 <= i < TILES or i % MT != MT - 1:
                return
            den = small.tile([P, MT], F32)
            nc.vector.reduce_sum(out=den[:], in_=live["e_sums", class_of(i)][:].rearrange("p s t -> p t s"), axis=AX.X)
            live["den", class_of(i)] = den

        def inverse(i):
            if not 0 <= i < TILES or i % MT != MT - 1:
                return
            inv_den = small.tile([P, MT], F32)
            nc.vector.reciprocal(out=inv_den[:], in_=live["den", class_of(i)][:])
            live["inv_den", class_of(i)] = inv_den

        def atrous_product(i):
            tiles = piece_of(i)
            if not tiles:
                return
            cls = class_of(i)
            e_codes, e_scales = live["e_codes", cls]
            atrous = psum_s.tile([P, MT, H], F32, tag="sum")
            for t in tiles:
                cols = slice(t * P, (t + 1) * P)
                nc.tensor.matmul_mx(
                    out=atrous[:, t, :],
                    lhsT=e_codes[:, cols].bitcast(FP8X4), lhsT_scale=e_scales[:, cols],
                    rhs=v_codes[:, cls, :].bitcast(FP8X4), rhs_scale=v_scales[:, cls, :],
                    start=True, stop=True,
                )
                live["atrous", cls, t] = atrous

        def add_local_first(i):
            if not 0 <= i < TILES:
                return
            cls, t = class_of(i), tile_of(i)
            b, r = cls // G, cls % G
            if i % MT == 0:
                with_one = pipe2.tile([P, MT, H], F32)
                live["with_one", cls] = with_one
            nc.vector.scalar_tensor_tensor(
                out=live["with_one", cls][:, t, :], in0=v_ext[:, b * MT + t, LW + r - 1, :],
                scalar=live["e_sums", cls][:, 1, t : t + 1], in1=live["atrous", cls, t][:, t, :], op0=ALU.mult, op1=ALU.add,
            )

        def add_local_second(i):
            if not 0 <= i < TILES:
                return
            cls, t = class_of(i), tile_of(i)
            b, r = cls // G, cls % G
            if i % MT == 0:
                with_two = pipe2.tile([P, MT, H], F32)
                live["with_two", cls] = with_two
            nc.vector.scalar_tensor_tensor(
                out=live["with_two", cls][:, t, :], in0=v_ext[:, b * MT + t, LW + r - 2, :],
                scalar=live["e_sums", cls][:, 2, t : t + 1], in1=live["with_one", cls][:, t, :], op0=ALU.mult, op1=ALU.add,
            )

        def divide(i):
            if not 0 <= i < TILES:
                return
            cls, t = class_of(i), tile_of(i)
            b, r = cls // G, cls % G
            if i % MT == 0:
                result = results.tile([P, MT, H], F32)
                live["result", cls] = result
            if i >= TILES - 2 * MT:
                nc.scalar.activation(
                    out=live["result", cls][:, t, :], in_=live["with_two", cls][:, t, :], func=ACT.Copy,
                    scale=live["inv_den", cls][:, t : t + 1],
                )
            else:
                nc.gpsimd.tensor_scalar(
                    out=live["result", cls][:, t, :], in0=live["with_two", cls][:, t, :],
                    scalar1=live["inv_den", cls][:, t : t + 1], scalar2=1.0, op0=ALU.mult, op1=ALU.mult,
                )
            tiles = piece_of(i)
            if tiles:
                t0, t1 = tiles[0], tiles[-1] + 1
                nc.sync.dma_start(out=out_tiles[r, :, b * MT + t0 : b * MT + t1, :], in_=live["result", cls][:, t0:t1, :])

        LAST = BEHIND + TILES + 14
        def run_step(step):
            i = step - FRONT_BEHIND
            j = step - BEHIND
            v_shift(step - 5)
            local_minimum(step)
            top(i - 1)
            add_local_first(j - 11)
            add_local_second(j - 12)
            divide(j - 13)
            logits(i)
            e_bank_zero(step)
            w_turn(step)
            x_turn(step)
            w_copy(step - 1)
            x_copy(step - 1)
            w_quantise(step - 2)
            x_quantise(step - 2)
            v_project(step - 3)
            atrous_product(j - 7)
            v_copy_rows(step - 4)
            v_copy_keys(step - 4)
            v_quantise(step - 5)
            local_logits(step)
            qk_turn(i + 4)
            qk_copy(i + 3)
            exponentials(i - 2)
            e_turn(i - 3)
            e_copy(i - 4)
            e_quantise(i - 5)
            local_shift(i - 2)
            local_exp(i - 3)
            denominator(i - 4)
            inverse(i - 5)

        with tc.manual_schedule():
            for step in range(FRONT_BEHIND):
                run_step(step)
        for step in range(FRONT_BEHIND, LAST):
            run_step(step)
